import numpy as np
import ml_dtypes


def mxq(x, axis, fmt="e4m3"):
    dtype, down = {"e4m3": (ml_dtypes.float8_e4m3fn, 7), "e5m2": (ml_dtypes.float8_e5m2, 14)}[fmt]
    v = np.moveaxis(np.asarray(x, np.float32).astype(ml_dtypes.bfloat16).astype(np.float64), axis, -1)
    blocks = v.reshape(v.shape[:-1] + (-1, 32))
    amax = np.abs(blocks).max(-1, keepdims=True)
    byte = np.maximum(np.where(amax > 0, np.frexp(amax)[1] - 1 + 127, 0) - down, 1)
    scale = np.exp2(byte - 127.0)
    codes = (blocks / scale).astype(np.float32).astype(dtype).astype(np.float64)
    return np.moveaxis((codes * scale).reshape(v.shape), -1, axis)


WIDE = False


def mx_kscale(k):
    if not WIDE:
        return np.ones(k)
    levels = np.array([10, -10, 5, -5, 0])
    a = np.random.permutation(np.resize(levels, k // 512 * 4)).reshape(k // 512, 4)
    idx = np.arange(k)
    return np.exp2(a[idx // 512, idx % 128 // 32])


BF16 = ml_dtypes.bfloat16


def bf(x):
    return np.asarray(x, np.float32).astype(BF16)


def f64(x):
    return np.asarray(x).astype(np.float64)


B, CIN, HID, FREQ, T, H = 1, 512, 512, 4, 512, 8
HD = HID * FREQ // H
EPS = 1e-5


def setup_inputs():
    s = mx_kscale(CIN)
    return {"x": bf(np.random.standard_normal((B, CIN, FREQ, T)) * s[None, :, None, None]),
            "qkv_w": bf(np.random.standard_normal((3 * HID, CIN)) / np.sqrt(CIN) / s[None, :]),
            "qkv_b": bf(np.random.standard_normal(3 * HID) * 0.2),
            "qkv_alpha": bf(0.25 + 0.05 * np.random.standard_normal(1)),
            "qkv_gamma": bf(1.0 + 0.1 * np.random.standard_normal((1, 3 * HID, 1, FREQ))),
            "qkv_beta": bf(0.1 * np.random.standard_normal((1, 3 * HID, 1, FREQ)))}


def reference(x, qkv_w, qkv_b, qkv_alpha, qkv_gamma, qkv_beta):
    xt = np.swapaxes(f64(x), -2, -1)
    y = (mxq(f64(qkv_w), 1, "e4m3") @ mxq(xt, 1, "e4m3").reshape(B, CIN, T * FREQ)).reshape(B, 3 * HID, T, FREQ)
    y = y + f64(qkv_b)[None, :, None, None]
    y = np.where(y >= 0, y, f64(qkv_alpha)[0] * y)
    mu = y.mean(axis=(1, 3), keepdims=True)
    var = np.square(y - mu).mean(axis=(1, 3), keepdims=True)
    n = (y - mu) / np.sqrt(var + EPS) * f64(qkv_gamma) + f64(qkv_beta)
    n = np.swapaxes(np.swapaxes(n, 1, 2).reshape(B, T, H, 3 * HD), 1, 2)
    return (np.ascontiguousarray(n[..., :HD]), np.ascontiguousarray(n[..., HD:2 * HD]), np.ascontiguousarray(n[..., 2 * HD:]))

@@ -1,0 +1,267 @@
+from contextlib import ExitStack
+
+import concourse.mybir as mybir
+from concourse.masks import make_identity
+
+F32 = mybir.dt.float32
+BF16 = mybir.dt.bfloat16
+U32 = mybir.dt.uint32
+U8 = mybir.dt.uint8
+FP8X4 = mybir.dt.float8_e4m3fn_x4
+ALU = mybir.AluOpType
+ACT = mybir.ActivationFunctionType
+AX = mybir.AxisListType
+
+P = 128
+PACK = 4
+CIN = 512
+COUT = 1536
+FREQ = 4
+T = 512
+HEADS = 8
+HEAD_DIM = 256
+EPS = 1e-5
+
+BANK = 512
+O_TILES = COUT // P
+T_BLOCKS = T // P
+ROW = COUT * FREQ
+W_CHUNK = 4
+STORE_TILES = 3
+STORE_COLS = STORE_TILES * BANK
+STORE_HEADS = STORE_COLS // (3 * HEAD_DIM)
+
+FLOPS = 2 * COUT * CIN * FREQ * T
+
+
+def tile_unified2dattentiononframe_pa_kernel(
+    tc, x, qkv_w, qkv_b, qkv_alpha, qkv_gamma, qkv_beta, out_0, out_1, out_2
+):
+    nc = tc.nc
+    outs = (out_0, out_1, out_2)
+
+    with ExitStack() as stack:
+        const = stack.enter_context(tc.tile_pool(name="const", bufs=1))
+        w_load = stack.enter_context(tc.tile_pool(name="w_load", bufs=3))
+        x_load = stack.enter_context(tc.tile_pool(name="x_load", bufs=T_BLOCKS))
+        group = stack.enter_context(tc.tile_pool(name="group", bufs=2))
+        signed_pool = stack.enter_context(tc.tile_pool(name="signed", bufs=3))
+        act_pool = stack.enter_context(tc.tile_pool(name="act", bufs=O_TILES + 6))
+        waste_pool = stack.enter_context(tc.tile_pool(name="waste", bufs=3))
+        norm_pool = stack.enter_context(tc.tile_pool(name="norm", bufs=9))
+        stat = stack.enter_context(tc.tile_pool(name="stat", bufs=3))
+        psum_mx = stack.enter_context(tc.psum_pool(name="psum_mx", bufs=2))
+        psum_sum = stack.enter_context(tc.psum_pool(name="psum_sum", bufs=2))
+        psum_flip = stack.enter_context(tc.psum_pool(name="psum_flip", bufs=4))
+
+        ident = const.tile([P, P], F32)
+        make_identity(nc, ident[:])
+
+        one = const.tile([P, 1], F32)
+        nc.vector.memset(one[:], 1.0)
+        one_root = const.tile([P, 1], F32)
+        nc.scalar.activation(out=one_root[:], in_=one[:], func=ACT.Sqrt)
+
+        alpha_bf = const.tile([P, 1], BF16)
+        nc.sync.dma_start(out=alpha_bf[:], in_=qkv_alpha.partition_broadcast(P))
+        bias_rows_bf = const.tile([P, P], BF16)
+        nc.vector.memset(bias_rows_bf[:], 0.0)
+        nc.sync.dma_start(out=bias_rows_bf[0:O_TILES, :], in_=qkv_b.rearrange("(a p) -> a p", p=P))
+
+        x_rows = x[0].rearrange("(p k) f t -> p (k f) t", k=PACK)
+        x_raw = []
+        w_raw = []
+
+        def load_x(tb):
+            raw = x_load.tile([P, PACK, BANK], BF16, name="x_raw")
+            nc.sync.dma_start(
+                out=raw[:].rearrange("p k (f t) -> p (k f) t", t=P),
+                in_=x_rows[:, :, tb * P : (tb + 1) * P],
+            )
+            x_raw.append(raw)
+
+        def load_w(chunk):
+            raw = w_load.tile([P, W_CHUNK, CIN], BF16, name="w_raw")
+            rows = qkv_w[chunk * W_CHUNK * P : (chunk + 1) * W_CHUNK * P, :]
+            nc.sync.dma_start(out=raw[:], in_=rows.rearrange("(a p) c -> p a c", p=P))
+            w_raw.append(raw)
+
+        gamma_bc = const.tile([P, ROW], BF16)
+        beta_bc = const.tile([P, ROW], BF16)
+        load_x(0)
+        load_w(0)
+        load_w(1)
+        load_w(2)
+        load_x(1)
+        nc.sync.dma_start(
+            out=gamma_bc[:], in_=qkv_gamma.rearrange("a o b f -> (a o b f)").partition_broadcast(P)
+        )
+        load_x(2)
+        load_x(3)
+        nc.sync.dma_start(
+            out=beta_bc[:], in_=qkv_beta.rearrange("a o b f -> (a o b f)").partition_broadcast(P)
+        )
+
+        alpha = const.tile([P, 1], F32)
+        nc.vector.tensor_copy(out=alpha[:], in_=alpha_bf[:])
+        sign = const.tile([P, 1], F32)
+        nc.vector.tensor_scalar(
+            out=sign[:], in0=alpha[:], scalar1=1.0, scalar2=-2.0, op0=ALU.is_gt, op1=ALU.mult
+        )
+        nc.vector.tensor_scalar_add(out=sign[:], in0=sign[:], scalar1=1.0)
+
+        bias_rows = const.tile([P, P], F32)
+        nc.vector.tensor_copy(out=bias_rows[:], in_=bias_rows_bf[:])
+        bias_cols = psum_flip.tile([P, P], F32, tag="flip")
+        nc.tensor.transpose(bias_cols[:], bias_rows[:], ident[:])
+        signed_bias = const.tile([P, O_TILES], F32)
+        nc.vector.tensor_scalar_mul(
+            out=signed_bias[:], in0=bias_cols[:, 0:O_TILES], scalar1=sign[:, 0:1]
+        )
+
+        w_codes = const.tile([P, COUT], U32, align_bytes=64)
+        w_scales = const.tile([P, COUT], U8, align_bytes=64)
+
+        def quantise_w(chunk):
+            words = w_raw[chunk][:].bitcast(F32).rearrange("p a (q u) -> p a u q", u=2)
+            grouped = group.tile([P, W_CHUNK * P, PACK], BF16, align_bytes=64, name="w_grouped")
+            grouped_words = grouped[:].bitcast(F32)
+            for half in range(2):
+                flipped = psum_flip.tile([P, 2, 2, P], F32, tag="flip", name="w_flipped")
+                for a in range(2):
+                    for u in range(2):
+                        nc.tensor.transpose(flipped[:, a, u, :], words[:, 2 * half + a, u, :], ident[:])
+                dst = grouped_words[:, 2 * half * P : (2 * half + 2) * P, :]
+                dst = dst.rearrange("p (a o) u -> p a o u", a=2)
+                src = flipped[:].rearrange("p a u o -> p a o u")
+                if half == 0:
+                    nc.scalar.copy(out=dst, in_=src)
+                else:
+                    nc.vector.tensor_copy(out=dst, in_=src)
+            cols = slice(chunk * W_CHUNK * P, (chunk + 1) * W_CHUNK * P)
+            nc.vector.quantize_mx(
+                out=w_codes[:, cols].bitcast(FP8X4),
+                scales=w_scales[:, cols],
+                in_=grouped[:].rearrange("p o k -> p (o k)"),
+            )
+
+        x_codes = const.tile([P, T_BLOCKS, BANK], U32, align_bytes=64)
+        x_scales = const.tile([P, T_BLOCKS, BANK], U8, align_bytes=64)
+
+        def quantise_x(tb):
+            grouped = group.tile([P, BANK, PACK], BF16, align_bytes=64, name="x_grouped")
+            nc.vector.tensor_copy(
+                out=grouped[:].rearrange("p (c i) k -> p c k i", i=4),
+                in_=x_raw[tb][:].rearrange("p k (c i) -> p c k i", i=4),
+            )
+            nc.vector.quantize_mx(
+                out=x_codes[:, tb, :].bitcast(FP8X4),
+                scales=x_scales[:, tb, :],
+                in_=grouped[:].rearrange("p n k -> p (n k)"),
+            )
+
+        quantise_w(0)
+        quantise_x(0)
+        quantise_w(1)
+        quantise_w(2)
+
+        for tb in range(T_BLOCKS):
+            if tb + 1 < T_BLOCKS:
+                quantise_x(tb + 1)
+
+            acts = []
+            row_sums = psum_sum.tile([P, P], F32)
+            for ot in range(O_TILES):
+                o_cols = slice(ot * P, (ot + 1) * P)
+                product = psum_mx.tile([P, BANK], F32)
+                nc.tensor.matmul_mx(
+                    out=product[:],
+                    lhsT=w_codes[:, o_cols].bitcast(FP8X4),
+                    lhsT_scale=w_scales[:, o_cols],
+                    rhs=x_codes[:, tb, :].bitcast(FP8X4),
+                    rhs_scale=x_scales[:, tb, :],
+                    start=True,
+                    stop=True,
+                )
+                signed = signed_pool.tile([P, BANK], F32)
+                nc.scalar.activation(
+                    out=signed[:],
+                    in_=product[:],
+                    func=ACT.Identity,
+                    bias=signed_bias[:, ot : ot + 1],
+                    scale=sign[:, 0:1],
+                )
+                act = act_pool.tile([P, BANK], F32)
+                nc.vector.scalar_tensor_tensor(
+                    out=act[:], in0=signed[:], scalar=alpha[:, 0:1], in1=signed[:], op0=ALU.mult, op1=ALU.max
+                )
+                acts.append(act)
+                for f in range(FREQ):
+                    nc.tensor.matmul(
+                        out=row_sums[:],
+                        lhsT=act[:, f * P : (f + 1) * P],
+                        rhs=ident[:],
+                        is_transpose=True,
+                        start=(ot == 0 and f == 0),
+                        stop=(ot == O_TILES - 1 and f == FREQ - 1),
+                    )
+
+            total = stat.tile([P, 1], F32)
+            nc.vector.tensor_reduce(out=total[:], in_=row_sums[:], axis=AX.X, op=ALU.add)
+            neg_mean = stat.tile([P, 1], F32)
+            nc.vector.tensor_scalar_mul(out=neg_mean[:], in0=total[:], scalar1=-1.0 / ROW)
+
+            square_sums = stat.tile([P, O_TILES], F32)
+            pieces = []
+            for ot in range(O_TILES):
+                flipped = psum_flip.tile([P, FREQ, P], F32, tag="flip")
+                for f in range(FREQ):
+                    nc.tensor.transpose(flipped[:, f, :], acts[ot][:, f * P : (f + 1) * P], ident[:])
+                waste = waste_pool.tile([P, BANK], BF16)
+                nc.scalar.activation(
+                    out=waste[:],
+                    in_=flipped[:].rearrange("p f o -> p (f o)"),
+                    func=ACT.Square,
+                    bias=neg_mean[:, 0:1],
+                    scale=1.0,
+                    accum_out=square_sums[:, ot : ot + 1],
+                )
+                if ot % STORE_TILES == 0:
+                    piece = norm_pool.tile([P, STORE_COLS], F32)
+                    pieces.append(piece)
+                part = slice((ot % STORE_TILES) * BANK, (ot % STORE_TILES + 1) * BANK)
+                nc.vector.scalar_tensor_tensor(
+                    out=pieces[-1][:, part].rearrange("p (o f) -> p o f", f=FREQ),
+                    in0=flipped[:].rearrange("p f o -> p o f"),
+                    scalar=neg_mean[:, 0:1],
+                    in1=gamma_bc[:, ot * BANK : (ot + 1) * BANK].rearrange("p (o f) -> p o f", f=FREQ),
+                    op0=ALU.add,
+                    op1=ALU.mult,
+                )
+
+            square_total = stat.tile([P, 1], F32)
+            nc.vector.tensor_reduce(out=square_total[:], in_=square_sums[:], axis=AX.X, op=ALU.add)
+            variance = stat.tile([P, 1], F32)
+            nc.vector.tensor_scalar(
+                out=variance[:], in0=square_total[:], scalar1=1.0 / ROW, scalar2=EPS, op0=ALU.mult, op1=ALU.add
+            )
+            deviation = stat.tile([P, 1], F32)
+            nc.scalar.activation(out=deviation[:], in_=variance[:], func=ACT.Sqrt)
+            rstd = stat.tile([P, 1], F32)
+            nc.vector.reciprocal(out=rstd[:], in_=deviation[:])
+            signed_rstd = stat.tile([P, 1], F32)
+            nc.vector.tensor_mul(out=signed_rstd[:], in0=rstd[:], in1=sign[:])
+
+            for s, piece in enumerate(pieces):
+                nc.vector.scalar_tensor_tensor(
+                    out=piece[:],
+                    in0=piece[:],
+                    scalar=signed_rstd[:, 0:1],
+                    in1=beta_bc[:, s * STORE_COLS : (s + 1) * STORE_COLS],
+                    op0=ALU.mult,
+                    op1=ALU.add,
+                )
+                split = piece[:].rearrange("p (h w d) -> p h w d", h=STORE_HEADS, w=3)
+                for w, out_w in enumerate(outs):
+                    rows = out_w[0, s * STORE_HEADS : (s + 1) * STORE_HEADS, tb * P : (tb + 1) * P, :]
+                    nc.sync.dma_start(out=rows.rearrange("h t d -> t h d"), in_=split[:, :, w, :])

@@ -27,9 +27,13 @@ O_TILES = COUT // P
 T_BLOCKS = T // P
 ROW = COUT * FREQ
 W_CHUNK = 4
-STORE_TILES = 3
-STORE_COLS = STORE_TILES * BANK
-STORE_HEADS = STORE_COLS // (3 * HEAD_DIM)
+PIECE_TILES = 3
+PIECE_COLS = PIECE_TILES * BANK
+PIECE_HEADS = PIECE_COLS // (3 * HEAD_DIM)
+BLOCK_PIECES = O_TILES // PIECE_TILES
+PIECES = T_BLOCKS * BLOCK_PIECES
+GAIN_LAG = BLOCK_PIECES + 1
+SHIFT_LAG = BLOCK_PIECES + 1
 
 FLOPS = 2 * COUT * CIN * FREQ * T
 
@@ -41,18 +45,19 @@ def tile_unified2dattentiononframe_pa_kernel(
     outs = (out_0, out_1, out_2)
 
     with ExitStack() as stack:
+        stack.enter_context(tc.manual_schedule())
         const = stack.enter_context(tc.tile_pool(name="const", bufs=1))
-        w_load = stack.enter_context(tc.tile_pool(name="w_load", bufs=3))
+        w_load = stack.enter_context(tc.tile_pool(name="w_load", bufs=COUT // (W_CHUNK * P)))
         x_load = stack.enter_context(tc.tile_pool(name="x_load", bufs=T_BLOCKS))
         group = stack.enter_context(tc.tile_pool(name="group", bufs=2))
-        signed_pool = stack.enter_context(tc.tile_pool(name="signed", bufs=3))
-        act_pool = stack.enter_context(tc.tile_pool(name="act", bufs=O_TILES + 6))
-        waste_pool = stack.enter_context(tc.tile_pool(name="waste", bufs=3))
-        norm_pool = stack.enter_context(tc.tile_pool(name="norm", bufs=9))
+        signed_pool = stack.enter_context(tc.tile_pool(name="signed", bufs=PIECE_TILES + 1))
+        act_pool = stack.enter_context(tc.tile_pool(name="act", bufs=(GAIN_LAG + 1) * PIECE_TILES))
+        waste_pool = stack.enter_context(tc.tile_pool(name="waste", bufs=PIECE_TILES))
+        norm_pool = stack.enter_context(tc.tile_pool(name="norm", bufs=SHIFT_LAG + 3))
         stat = stack.enter_context(tc.tile_pool(name="stat", bufs=3))
-        psum_mx = stack.enter_context(tc.psum_pool(name="psum_mx", bufs=2))
-        psum_sum = stack.enter_context(tc.psum_pool(name="psum_sum", bufs=2))
-        psum_flip = stack.enter_context(tc.psum_pool(name="psum_flip", bufs=4))
+        psum_mx = stack.enter_context(tc.psum_pool(name="psum_mx", bufs=PIECE_TILES))
+        psum_sum = stack.enter_context(tc.psum_pool(name="psum_sum", bufs=1))
+        psum_flip = stack.enter_context(tc.psum_pool(name="psum_flip", bufs=PIECE_TILES + 1))
 
         ident = const.tile([P, P], F32)
         make_identity(nc, ident[:])
@@ -88,16 +93,16 @@ def tile_unified2dattentiononframe_pa_kernel(
 
         gamma_bc = const.tile([P, ROW], BF16)
         beta_bc = const.tile([P, ROW], BF16)
-        load_x(0)
         load_w(0)
+        load_x(0)
         load_w(1)
         load_w(2)
         load_x(1)
+        load_x(2)
+        load_x(3)
         nc.sync.dma_start(
             out=gamma_bc[:], in_=qkv_gamma.rearrange("a o b f -> (a o b f)").partition_broadcast(P)
         )
-        load_x(2)
-        load_x(3)
         nc.sync.dma_start(
             out=beta_bc[:], in_=qkv_beta.rearrange("a o b f -> (a o b f)").partition_broadcast(P)
         )
@@ -122,7 +127,7 @@ def tile_unified2dattentiononframe_pa_kernel(
         w_codes = const.tile([P, COUT], U32, align_bytes=64)
         w_scales = const.tile([P, COUT], U8, align_bytes=64)
 
-        def quantise_w(chunk):
+        def quantise_w(chunk, copy_out):
             words = w_raw[chunk][:].bitcast(F32).rearrange("p a (q u) -> p a u q", u=2)
             grouped = group.tile([P, W_CHUNK * P, PACK], BF16, align_bytes=64, name="w_grouped")
             grouped_words = grouped[:].bitcast(F32)
@@ -132,12 +137,10 @@ def tile_unified2dattentiononframe_pa_kernel(
                     for u in range(2):
                         nc.tensor.transpose(flipped[:, a, u, :], words[:, 2 * half + a, u, :], ident[:])
                 dst = grouped_words[:, 2 * half * P : (2 * half + 2) * P, :]
-                dst = dst.rearrange("p (a o) u -> p a o u", a=2)
-                src = flipped[:].rearrange("p a u o -> p a o u")
-                if half == 0:
-                    nc.scalar.copy(out=dst, in_=src)
-                else:
-                    nc.vector.tensor_copy(out=dst, in_=src)
+                copy_out(
+                    out=dst.rearrange("p (a o) u -> p a o u", a=2),
+                    in_=flipped[:].rearrange("p a u o -> p a o u"),
+                )
             cols = slice(chunk * W_CHUNK * P, (chunk + 1) * W_CHUNK * P)
             nc.vector.quantize_mx(
                 out=w_codes[:, cols].bitcast(FP8X4),
@@ -160,18 +163,20 @@ def tile_unified2dattentiononframe_pa_kernel(
                 in_=grouped[:].rearrange("p n k -> p (n k)"),
             )
 
-        quantise_w(0)
-        quantise_x(0)
-        quantise_w(1)
-        quantise_w(2)
+        products = {}
+        acts = {}
+        flips = {}
+        norms = {}
+        row_sums = {}
+        neg_mean = {}
+        square_sums = {}
+        variance = {}
+        signed_rstd = {}
 
-        for tb in range(T_BLOCKS):
-            if tb + 1 < T_BLOCKS:
-                quantise_x(tb + 1)
-
-            acts = []
-            row_sums = psum_sum.tile([P, P], F32)
-            for ot in range(O_TILES):
+        def multiply(piece):
+            tb = piece // BLOCK_PIECES
+            for i in range(PIECE_TILES):
+                ot = (piece % BLOCK_PIECES) * PIECE_TILES + i
                 o_cols = slice(ot * P, (ot + 1) * P)
                 product = psum_mx.tile([P, BANK], F32)
                 nc.tensor.matmul_mx(
@@ -183,10 +188,15 @@ def tile_unified2dattentiononframe_pa_kernel(
                     start=True,
                     stop=True,
                 )
+                products[(piece, i)] = product
+
+        def bias_prelu(piece):
+            for i in range(PIECE_TILES):
+                ot = (piece % BLOCK_PIECES) * PIECE_TILES + i
                 signed = signed_pool.tile([P, BANK], F32)
                 nc.scalar.activation(
                     out=signed[:],
-                    in_=product[:],
+                    in_=products[(piece, i)][:],
                     func=ACT.Identity,
                     bias=signed_bias[:, ot : ot + 1],
                     scale=sign[:, 0:1],
@@ -195,73 +205,119 @@ def tile_unified2dattentiononframe_pa_kernel(
                 nc.vector.scalar_tensor_tensor(
                     out=act[:], in0=signed[:], scalar=alpha[:, 0:1], in1=signed[:], op0=ALU.mult, op1=ALU.max
                 )
-                acts.append(act)
+                acts[(piece, i)] = act
+
+        def add_to_row_sums(piece):
+            tb = piece // BLOCK_PIECES
+            if piece % BLOCK_PIECES == 0:
+                row_sums[tb] = psum_sum.tile([P, P], F32, name="row_sums")
+            for i in range(PIECE_TILES):
                 for f in range(FREQ):
                     nc.tensor.matmul(
-                        out=row_sums[:],
-                        lhsT=act[:, f * P : (f + 1) * P],
+                        out=row_sums[tb][:],
+                        lhsT=acts[(piece, i)][:, f * P : (f + 1) * P],
                         rhs=ident[:],
                         is_transpose=True,
-                        start=(ot == 0 and f == 0),
-                        stop=(ot == O_TILES - 1 and f == FREQ - 1),
+                        start=(piece % BLOCK_PIECES == 0 and i == 0 and f == 0),
+                        stop=(piece % BLOCK_PIECES == BLOCK_PIECES - 1 and i == PIECE_TILES - 1 and f == FREQ - 1),
                     )
 
+        def mean_of_block(tb):
             total = stat.tile([P, 1], F32)
-            nc.vector.tensor_reduce(out=total[:], in_=row_sums[:], axis=AX.X, op=ALU.add)
-            neg_mean = stat.tile([P, 1], F32)
-            nc.vector.tensor_scalar_mul(out=neg_mean[:], in0=total[:], scalar1=-1.0 / ROW)
+            nc.vector.tensor_reduce(out=total[:], in_=row_sums[tb][:], axis=AX.X, op=ALU.add)
+            neg_mean[tb] = stat.tile([P, 1], F32, name="neg_mean")
+            nc.vector.tensor_scalar_mul(out=neg_mean[tb][:], in0=total[:], scalar1=-1.0 / ROW)
+            square_sums[tb] = stat.tile([P, O_TILES], F32, name="square_sums")
 
-            square_sums = stat.tile([P, O_TILES], F32)
-            pieces = []
-            for ot in range(O_TILES):
+        def flip(piece):
+            for i in range(PIECE_TILES):
                 flipped = psum_flip.tile([P, FREQ, P], F32, tag="flip")
                 for f in range(FREQ):
-                    nc.tensor.transpose(flipped[:, f, :], acts[ot][:, f * P : (f + 1) * P], ident[:])
+                    nc.tensor.transpose(flipped[:, f, :], acts[(piece, i)][:, f * P : (f + 1) * P], ident[:])
+                flips[(piece, i)] = flipped
+
+        def square_gain(piece):
+            tb = piece // BLOCK_PIECES
+            norms[piece] = norm_pool.tile([P, PIECE_COLS], F32, name="norm")
+            for i in range(PIECE_TILES):
+                ot = (piece % BLOCK_PIECES) * PIECE_TILES + i
+                flipped = flips[(piece, i)]
                 waste = waste_pool.tile([P, BANK], BF16)
                 nc.scalar.activation(
                     out=waste[:],
                     in_=flipped[:].rearrange("p f o -> p (f o)"),
                     func=ACT.Square,
-                    bias=neg_mean[:, 0:1],
+                    bias=neg_mean[tb][:, 0:1],
                     scale=1.0,
-                    accum_out=square_sums[:, ot : ot + 1],
+                    accum_out=square_sums[tb][:, ot : ot + 1],
                 )
-                if ot % STORE_TILES == 0:
-                    piece = norm_pool.tile([P, STORE_COLS], F32)
-                    pieces.append(piece)
-                part = slice((ot % STORE_TILES) * BANK, (ot % STORE_TILES + 1) * BANK)
                 nc.vector.scalar_tensor_tensor(
-                    out=pieces[-1][:, part].rearrange("p (o f) -> p o f", f=FREQ),
+                    out=norms[piece][:, i * BANK : (i + 1) * BANK].rearrange("p (o f) -> p o f", f=FREQ),
                     in0=flipped[:].rearrange("p f o -> p o f"),
-                    scalar=neg_mean[:, 0:1],
+                    scalar=neg_mean[tb][:, 0:1],
                     in1=gamma_bc[:, ot * BANK : (ot + 1) * BANK].rearrange("p (o f) -> p o f", f=FREQ),
                     op0=ALU.add,
                     op1=ALU.mult,
                 )
 
+        def variance_of_block(tb):
             square_total = stat.tile([P, 1], F32)
-            nc.vector.tensor_reduce(out=square_total[:], in_=square_sums[:], axis=AX.X, op=ALU.add)
-            variance = stat.tile([P, 1], F32)
+            nc.vector.tensor_reduce(out=square_total[:], in_=square_sums[tb][:], axis=AX.X, op=ALU.add)
+            variance[tb] = stat.tile([P, 1], F32, name="variance")
             nc.vector.tensor_scalar(
-                out=variance[:], in0=square_total[:], scalar1=1.0 / ROW, scalar2=EPS, op0=ALU.mult, op1=ALU.add
+                out=variance[tb][:], in0=square_total[:], scalar1=1.0 / ROW, scalar2=EPS, op0=ALU.mult, op1=ALU.add
             )
+
+        def rstd_of_block(tb):
             deviation = stat.tile([P, 1], F32)
-            nc.scalar.activation(out=deviation[:], in_=variance[:], func=ACT.Sqrt)
+            nc.scalar.activation(out=deviation[:], in_=variance[tb][:], func=ACT.Sqrt)
             rstd = stat.tile([P, 1], F32)
             nc.vector.reciprocal(out=rstd[:], in_=deviation[:])
-            signed_rstd = stat.tile([P, 1], F32)
-            nc.vector.tensor_mul(out=signed_rstd[:], in0=rstd[:], in1=sign[:])
+            signed_rstd[tb] = stat.tile([P, 1], F32, name="signed_rstd")
+            nc.vector.tensor_mul(out=signed_rstd[tb][:], in0=rstd[:], in1=sign[:])
 
-            for s, piece in enumerate(pieces):
-                nc.vector.scalar_tensor_tensor(
-                    out=piece[:],
-                    in0=piece[:],
-                    scalar=signed_rstd[:, 0:1],
-                    in1=beta_bc[:, s * STORE_COLS : (s + 1) * STORE_COLS],
-                    op0=ALU.mult,
-                    op1=ALU.add,
-                )
-                split = piece[:].rearrange("p (h w d) -> p h w d", h=STORE_HEADS, w=3)
-                for w, out_w in enumerate(outs):
-                    rows = out_w[0, s * STORE_HEADS : (s + 1) * STORE_HEADS, tb * P : (tb + 1) * P, :]
-                    nc.sync.dma_start(out=rows.rearrange("h t d -> t h d"), in_=split[:, :, w, :])
+        def scale_shift_store(piece):
+            tb = piece // BLOCK_PIECES
+            s = piece % BLOCK_PIECES
+            norm = norms[piece]
+            nc.vector.scalar_tensor_tensor(
+                out=norm[:],
+                in0=norm[:],
+                scalar=signed_rstd[tb][:, 0:1],
+                in1=beta_bc[:, s * PIECE_COLS : (s + 1) * PIECE_COLS],
+                op0=ALU.mult,
+                op1=ALU.add,
+            )
+            split = norm[:].rearrange("p (h w d) -> p h w d", h=PIECE_HEADS, w=3)
+            for w, out_w in enumerate(outs):
+                rows = out_w[0, s * PIECE_HEADS : (s + 1) * PIECE_HEADS, tb * P : (tb + 1) * P, :]
+                nc.sync.dma_start(out=rows.rearrange("h t d -> t h d"), in_=split[:, :, w, :])
+
+        quantise_w(0, nc.scalar.copy)
+        quantise_x(0)
+        multiply(0)
+        for step in range(PIECES + GAIN_LAG + SHIFT_LAG):
+            gained = step - GAIN_LAG
+            shifted = gained - SHIFT_LAG
+            if 0 <= shifted:
+                scale_shift_store(shifted)
+            if 0 <= gained < PIECES:
+                flip(gained)
+            if 1 <= step <= PIECES:
+                add_to_row_sums(step - 1)
+            if step < PIECES:
+                bias_prelu(step)
+            if 1 <= step <= PIECES and step % BLOCK_PIECES == 0:
+                mean_of_block(step // BLOCK_PIECES - 1)
+            if 0 <= gained < PIECES:
+                square_gain(gained)
+            if step + 1 < COUT // (W_CHUNK * P):
+                quantise_w(step + 1, nc.vector.tensor_copy)
+            elif step < COUT // (W_CHUNK * P) + T_BLOCKS - 2:
+                quantise_x(step + 2 - COUT // (W_CHUNK * P))
+            if step + 1 < PIECES:
+                multiply(step + 1)
+            if 0 <= gained < PIECES and gained % BLOCK_PIECES == BLOCK_PIECES - 1:
+                variance_of_block(gained // BLOCK_PIECES)
+            if 1 <= gained <= PIECES and gained % BLOCK_PIECES == 0:
+                rstd_of_block(gained // BLOCK_PIECES - 1)

@@ -30,10 +30,19 @@ W_CHUNK = 4
 PIECE_TILES = 3
 PIECE_COLS = PIECE_TILES * BANK
 PIECE_HEADS = PIECE_COLS // (3 * HEAD_DIM)
-BLOCK_PIECES = O_TILES // PIECE_TILES
-PIECES = T_BLOCKS * BLOCK_PIECES
-GAIN_LAG = BLOCK_PIECES + 1
-SHIFT_LAG = BLOCK_PIECES + 1
+TILES = T_BLOCKS * O_TILES
+
+AT_BIAS = 1
+AT_PRELU = 2
+AT_SUM = 3
+AT_MEAN = 4
+AT_SQUARE = O_TILES + AT_MEAN
+AT_FLIP = AT_SQUARE - 1
+AT_GAIN = AT_SQUARE + 1
+AT_RSTD = AT_SQUARE + 1
+AT_SHIFT = AT_RSTD + 1 + O_TILES - PIECE_TILES
+STEPS = TILES + AT_SHIFT
+PRODUCT_REPEATS = 2
 
 FLOPS = 2 * COUT * CIN * FREQ * T
 
@@ -50,14 +59,14 @@ def tile_unified2dattentiononframe_pa_kernel(
         w_load = stack.enter_context(tc.tile_pool(name="w_load", bufs=COUT // (W_CHUNK * P)))
         x_load = stack.enter_context(tc.tile_pool(name="x_load", bufs=T_BLOCKS))
         group = stack.enter_context(tc.tile_pool(name="group", bufs=2))
-        signed_pool = stack.enter_context(tc.tile_pool(name="signed", bufs=PIECE_TILES + 1))
-        act_pool = stack.enter_context(tc.tile_pool(name="act", bufs=(GAIN_LAG + 1) * PIECE_TILES))
-        waste_pool = stack.enter_context(tc.tile_pool(name="waste", bufs=PIECE_TILES))
-        norm_pool = stack.enter_context(tc.tile_pool(name="norm", bufs=SHIFT_LAG + 3))
+        signed_pool = stack.enter_context(tc.tile_pool(name="signed", bufs=3))
+        act_pool = stack.enter_context(tc.tile_pool(name="act", bufs=AT_FLIP - AT_PRELU + 2))
+        waste_pool = stack.enter_context(tc.tile_pool(name="waste", bufs=3))
+        norm_pool = stack.enter_context(tc.tile_pool(name="norm", bufs=7))
         stat = stack.enter_context(tc.tile_pool(name="stat", bufs=3))
-        psum_mx = stack.enter_context(tc.psum_pool(name="psum_mx", bufs=PIECE_TILES))
-        psum_sum = stack.enter_context(tc.psum_pool(name="psum_sum", bufs=1))
-        psum_flip = stack.enter_context(tc.psum_pool(name="psum_flip", bufs=PIECE_TILES + 1))
+        psum_mx = stack.enter_context(tc.psum_pool(name="psum_mx", bufs=2))
+        psum_sum = stack.enter_context(tc.psum_pool(name="psum_sum", bufs=2))
+        psum_flip = stack.enter_context(tc.psum_pool(name="psum_flip", bufs=4))
 
         ident = const.tile([P, P], F32)
         make_identity(nc, ident[:])
@@ -66,6 +75,9 @@ def tile_unified2dattentiononframe_pa_kernel(
         nc.vector.memset(one[:], 1.0)
         one_root = const.tile([P, 1], F32)
         nc.scalar.activation(out=one_root[:], in_=one[:], func=ACT.Sqrt)
+
+        eps = const.tile([P, 1], F32)
+        nc.vector.memset(eps[:], EPS)
 
         alpha_bf = const.tile([P, 1], BF16)
         nc.sync.dma_start(out=alpha_bf[:], in_=qkv_alpha.partition_broadcast(P))
@@ -164,121 +176,116 @@ def tile_unified2dattentiononframe_pa_kernel(
             )
 
         products = {}
+        signeds = {}
         acts = {}
         flips = {}
         norms = {}
         row_sums = {}
         neg_mean = {}
         square_sums = {}
-        variance = {}
+        signed_deviation = {}
         signed_rstd = {}
 
-        def multiply(piece):
-            tb = piece // BLOCK_PIECES
-            for i in range(PIECE_TILES):
-                ot = (piece % BLOCK_PIECES) * PIECE_TILES + i
-                o_cols = slice(ot * P, (ot + 1) * P)
-                product = psum_mx.tile([P, BANK], F32)
+        def multiply(g):
+            o_cols = slice((g % O_TILES) * P, (g % O_TILES + 1) * P)
+            products[g] = psum_mx.tile([P, BANK], F32, name="product")
+            for repeat in range(PRODUCT_REPEATS):
                 nc.tensor.matmul_mx(
-                    out=product[:],
+                    out=products[g][:],
                     lhsT=w_codes[:, o_cols].bitcast(FP8X4),
                     lhsT_scale=w_scales[:, o_cols],
-                    rhs=x_codes[:, tb, :].bitcast(FP8X4),
-                    rhs_scale=x_scales[:, tb, :],
+                    rhs=x_codes[:, g // O_TILES, :].bitcast(FP8X4),
+                    rhs_scale=x_scales[:, g // O_TILES, :],
                     start=True,
                     stop=True,
                 )
-                products[(piece, i)] = product
 
-        def bias_prelu(piece):
-            for i in range(PIECE_TILES):
-                ot = (piece % BLOCK_PIECES) * PIECE_TILES + i
-                signed = signed_pool.tile([P, BANK], F32)
-                nc.scalar.activation(
-                    out=signed[:],
-                    in_=products[(piece, i)][:],
-                    func=ACT.Identity,
-                    bias=signed_bias[:, ot : ot + 1],
-                    scale=sign[:, 0:1],
-                )
-                act = act_pool.tile([P, BANK], F32)
-                nc.vector.scalar_tensor_tensor(
-                    out=act[:], in0=signed[:], scalar=alpha[:, 0:1], in1=signed[:], op0=ALU.mult, op1=ALU.max
-                )
-                acts[(piece, i)] = act
-
-        def add_to_row_sums(piece):
-            tb = piece // BLOCK_PIECES
-            if piece % BLOCK_PIECES == 0:
-                row_sums[tb] = psum_sum.tile([P, P], F32, name="row_sums")
-            for i in range(PIECE_TILES):
-                for f in range(FREQ):
-                    nc.tensor.matmul(
-                        out=row_sums[tb][:],
-                        lhsT=acts[(piece, i)][:, f * P : (f + 1) * P],
-                        rhs=ident[:],
-                        is_transpose=True,
-                        start=(piece % BLOCK_PIECES == 0 and i == 0 and f == 0),
-                        stop=(piece % BLOCK_PIECES == BLOCK_PIECES - 1 and i == PIECE_TILES - 1 and f == FREQ - 1),
-                    )
-
-        def mean_of_block(tb):
-            total = stat.tile([P, 1], F32)
-            nc.vector.tensor_reduce(out=total[:], in_=row_sums[tb][:], axis=AX.X, op=ALU.add)
-            neg_mean[tb] = stat.tile([P, 1], F32, name="neg_mean")
-            nc.vector.tensor_scalar_mul(out=neg_mean[tb][:], in0=total[:], scalar1=-1.0 / ROW)
-            square_sums[tb] = stat.tile([P, O_TILES], F32, name="square_sums")
-
-        def flip(piece):
-            for i in range(PIECE_TILES):
-                flipped = psum_flip.tile([P, FREQ, P], F32, tag="flip")
-                for f in range(FREQ):
-                    nc.tensor.transpose(flipped[:, f, :], acts[(piece, i)][:, f * P : (f + 1) * P], ident[:])
-                flips[(piece, i)] = flipped
-
-        def square_gain(piece):
-            tb = piece // BLOCK_PIECES
-            norms[piece] = norm_pool.tile([P, PIECE_COLS], F32, name="norm")
-            for i in range(PIECE_TILES):
-                ot = (piece % BLOCK_PIECES) * PIECE_TILES + i
-                flipped = flips[(piece, i)]
-                waste = waste_pool.tile([P, BANK], BF16)
-                nc.scalar.activation(
-                    out=waste[:],
-                    in_=flipped[:].rearrange("p f o -> p (f o)"),
-                    func=ACT.Square,
-                    bias=neg_mean[tb][:, 0:1],
-                    scale=1.0,
-                    accum_out=square_sums[tb][:, ot : ot + 1],
-                )
-                nc.vector.scalar_tensor_tensor(
-                    out=norms[piece][:, i * BANK : (i + 1) * BANK].rearrange("p (o f) -> p o f", f=FREQ),
-                    in0=flipped[:].rearrange("p f o -> p o f"),
-                    scalar=neg_mean[tb][:, 0:1],
-                    in1=gamma_bc[:, ot * BANK : (ot + 1) * BANK].rearrange("p (o f) -> p o f", f=FREQ),
-                    op0=ALU.add,
-                    op1=ALU.mult,
-                )
-
-        def variance_of_block(tb):
-            square_total = stat.tile([P, 1], F32)
-            nc.vector.tensor_reduce(out=square_total[:], in_=square_sums[tb][:], axis=AX.X, op=ALU.add)
-            variance[tb] = stat.tile([P, 1], F32, name="variance")
-            nc.vector.tensor_scalar(
-                out=variance[tb][:], in0=square_total[:], scalar1=1.0 / ROW, scalar2=EPS, op0=ALU.mult, op1=ALU.add
+        def add_bias(g):
+            signeds[g] = signed_pool.tile([P, BANK], F32, name="signed")
+            nc.scalar.activation(
+                out=signeds[g][:],
+                in_=products[g][:],
+                func=ACT.Identity,
+                bias=signed_bias[:, g % O_TILES : g % O_TILES + 1],
+                scale=sign[:, 0:1],
             )
 
-        def rstd_of_block(tb):
+        def prelu(g):
+            acts[g] = act_pool.tile([P, BANK], F32, name="act")
+            nc.vector.scalar_tensor_tensor(
+                out=acts[g][:], in0=signeds[g][:], scalar=alpha[:, 0:1], in1=signeds[g][:], op0=ALU.mult, op1=ALU.max
+            )
+
+        def add_to_row_sums(g):
+            tb = g // O_TILES
+            if g % O_TILES == 0:
+                row_sums[tb] = psum_sum.tile([P, P], F32, name="row_sums")
+            for f in range(FREQ):
+                nc.tensor.matmul(
+                    out=row_sums[tb][:],
+                    lhsT=acts[g][:, f * P : (f + 1) * P],
+                    rhs=ident[:],
+                    is_transpose=True,
+                    start=(g % O_TILES == 0 and f == 0),
+                    stop=(g % O_TILES == O_TILES - 1 and f == FREQ - 1),
+                )
+
+        def mean_of_block(tb):
+            waste = waste_pool.tile([P, P], BF16, name="waste_mean")
+            neg_mean[tb] = stat.tile([P, 1], F32, name="neg_mean")
+            nc.scalar.activation(
+                out=waste[:], in_=row_sums[tb][:], func=ACT.Copy, scale=-1.0 / ROW, accum_out=neg_mean[tb][:]
+            )
+            square_sums[tb] = stat.tile([P, O_TILES], F32, name="square_sums")
+
+        def flip(g):
+            flips[g] = psum_flip.tile([P, FREQ, P], F32, tag="flip", name="flipped")
+            for f in range(FREQ):
+                nc.tensor.transpose(flips[g][:, f, :], acts[g][:, f * P : (f + 1) * P], ident[:])
+
+        def square(g):
+            waste = waste_pool.tile([P, BANK], BF16)
+            nc.scalar.activation(
+                out=waste[:],
+                in_=flips[g][:].rearrange("p f o -> p (f o)"),
+                func=ACT.Square,
+                bias=neg_mean[g // O_TILES][:, 0:1],
+                scale=1.0,
+                accum_out=square_sums[g // O_TILES][:, g % O_TILES : g % O_TILES + 1],
+            )
+
+        def gain(g):
+            if g % PIECE_TILES == 0:
+                norms[g // PIECE_TILES] = norm_pool.tile([P, PIECE_COLS], F32, name="norm")
+            part = slice((g % PIECE_TILES) * BANK, (g % PIECE_TILES + 1) * BANK)
+            gamma_part = gamma_bc[:, (g % O_TILES) * BANK : (g % O_TILES + 1) * BANK]
+            nc.vector.scalar_tensor_tensor(
+                out=norms[g // PIECE_TILES][:, part].rearrange("p (o f) -> p o f", f=FREQ),
+                in0=flips[g][:].rearrange("p f o -> p o f"),
+                scalar=neg_mean[g // O_TILES][:, 0:1],
+                in1=gamma_part.rearrange("p (o f) -> p o f", f=FREQ),
+                op0=ALU.add,
+                op1=ALU.mult,
+            )
+
+        def deviation_of_block(tb):
+            waste = waste_pool.tile([P, O_TILES], BF16, name="waste_variance")
+            variance = stat.tile([P, 1], F32)
+            nc.scalar.activation(
+                out=waste[:], in_=square_sums[tb][:], func=ACT.Copy, scale=1.0 / ROW, accum_out=variance[:]
+            )
             deviation = stat.tile([P, 1], F32)
-            nc.scalar.activation(out=deviation[:], in_=variance[tb][:], func=ACT.Sqrt)
-            rstd = stat.tile([P, 1], F32)
-            nc.vector.reciprocal(out=rstd[:], in_=deviation[:])
+            nc.scalar.activation(out=deviation[:], in_=variance[:], func=ACT.Sqrt, bias=eps[:, 0:1], scale=1.0)
+            signed_deviation[tb] = stat.tile([P, 1], F32, name="signed_deviation")
+            nc.scalar.activation(out=signed_deviation[tb][:], in_=deviation[:], func=ACT.Copy, scale=sign[:, 0:1])
+
+        def rstd_of_block(tb):
             signed_rstd[tb] = stat.tile([P, 1], F32, name="signed_rstd")
-            nc.vector.tensor_mul(out=signed_rstd[tb][:], in0=rstd[:], in1=sign[:])
+            nc.vector.reciprocal(out=signed_rstd[tb][:], in_=signed_deviation[tb][:])
 
         def scale_shift_store(piece):
-            tb = piece // BLOCK_PIECES
-            s = piece % BLOCK_PIECES
+            tb = piece // (O_TILES // PIECE_TILES)
+            s = piece % (O_TILES // PIECE_TILES)
             norm = norms[piece]
             nc.vector.scalar_tensor_tensor(
                 out=norm[:],
@@ -293,31 +300,41 @@ def tile_unified2dattentiononframe_pa_kernel(
                 rows = out_w[0, s * PIECE_HEADS : (s + 1) * PIECE_HEADS, tb * P : (tb + 1) * P, :]
                 nc.sync.dma_start(out=rows.rearrange("h t d -> t h d"), in_=split[:, :, w, :])
 
+        def is_tile(g):
+            return 0 <= g < TILES
+
+        def ends_block(g):
+            return is_tile(g) and g % O_TILES == O_TILES - 1
+
+        def ends_piece(g):
+            return is_tile(g) and g % PIECE_TILES == PIECE_TILES - 1
+
         quantise_w(0, nc.scalar.copy)
         quantise_x(0)
-        multiply(0)
-        for step in range(PIECES + GAIN_LAG + SHIFT_LAG):
-            gained = step - GAIN_LAG
-            shifted = gained - SHIFT_LAG
-            if 0 <= shifted:
-                scale_shift_store(shifted)
-            if 0 <= gained < PIECES:
-                flip(gained)
-            if 1 <= step <= PIECES:
-                add_to_row_sums(step - 1)
-            if step < PIECES:
-                bias_prelu(step)
-            if 1 <= step <= PIECES and step % BLOCK_PIECES == 0:
-                mean_of_block(step // BLOCK_PIECES - 1)
-            if 0 <= gained < PIECES:
-                square_gain(gained)
-            if step + 1 < COUT // (W_CHUNK * P):
-                quantise_w(step + 1, nc.vector.tensor_copy)
-            elif step < COUT // (W_CHUNK * P) + T_BLOCKS - 2:
-                quantise_x(step + 2 - COUT // (W_CHUNK * P))
-            if step + 1 < PIECES:
-                multiply(step + 1)
-            if 0 <= gained < PIECES and gained % BLOCK_PIECES == BLOCK_PIECES - 1:
-                variance_of_block(gained // BLOCK_PIECES)
-            if 1 <= gained <= PIECES and gained % BLOCK_PIECES == 0:
-                rstd_of_block(gained // BLOCK_PIECES - 1)
+        for n in range(STEPS):
+            if is_tile(n - AT_FLIP):
+                flip(n - AT_FLIP)
+            if is_tile(n - AT_SUM):
+                add_to_row_sums(n - AT_SUM)
+            if is_tile(n):
+                multiply(n)
+            if is_tile(n - AT_BIAS):
+                add_bias(n - AT_BIAS)
+            if is_tile(n - AT_SQUARE):
+                square(n - AT_SQUARE)
+            if ends_block(n - AT_SQUARE):
+                deviation_of_block((n - AT_SQUARE) // O_TILES)
+            if ends_block(n - AT_MEAN):
+                mean_of_block((n - AT_MEAN) // O_TILES)
+            if is_tile(n - AT_PRELU):
+                prelu(n - AT_PRELU)
+            if is_tile(n - AT_GAIN):
+                gain(n - AT_GAIN)
+            if ends_block(n - AT_RSTD):
+                rstd_of_block((n - AT_RSTD) // O_TILES)
+            if ends_piece(n - AT_SHIFT):
+                scale_shift_store((n - AT_SHIFT) // PIECE_TILES)
+            if n == 0 or n == 2:
+                quantise_w(n // 2 + 1, nc.vector.tensor_copy)
+            if n == 4 or n == 6 or n == 8:
+                quantise_x(n // 2 - 1)

@@ -10,7 +10,6 @@ U8 = mybir.dt.uint8
 FP8X4 = mybir.dt.float8_e4m3fn_x4
 ALU = mybir.AluOpType
 ACT = mybir.ActivationFunctionType
-AX = mybir.AxisListType
 
 P = 128
 PACK = 4
@@ -21,30 +20,29 @@ T = 512
 HEADS = 8
 HEAD_DIM = 256
 EPS = 1e-5
-
 BANK = 512
 O_TILES = COUT // P
 T_BLOCKS = T // P
 ROW = COUT * FREQ
-W_CHUNK = 4
 PIECE_TILES = 3
 PIECE_COLS = PIECE_TILES * BANK
 PIECE_HEADS = PIECE_COLS // (3 * HEAD_DIM)
 TILES = T_BLOCKS * O_TILES
-
-AT_BIAS = 1
-AT_PRELU = 2
-AT_SUM = 3
-AT_MEAN = 4
-AT_SQUARE = O_TILES + AT_MEAN
-AT_FLIP = AT_SQUARE - 1
-AT_GAIN = AT_SQUARE + 1
-AT_RSTD = AT_SQUARE + 1
-AT_SHIFT = AT_RSTD + 1 + O_TILES - PIECE_TILES
-STEPS = TILES + AT_SHIFT
-PRODUCT_REPEATS = 2
-
 FLOPS = 2 * COUT * CIN * FREQ * T
+
+W_GROUPS = (1,1,2,2,2,2,2)
+AT_BIAS = 1
+AT_PRELU = 3
+AT_SUM = 5
+AT_MEAN = 6
+AT_FLIP = O_TILES + AT_MEAN - 1 + 0
+AT_SQUARE = AT_FLIP + 1
+AT_GAIN = AT_FLIP + 2
+AT_RSTD = AT_SQUARE + 2
+TG = 1
+AT_SHIFT = 1
+XS = lambda nc, b: [nc.scalar.copy, nc.vector.tensor_copy]
+XPOS = (7,12,17)
 
 
 def tile_unified2dattentiononframe_pa_kernel(
@@ -56,123 +54,129 @@ def tile_unified2dattentiononframe_pa_kernel(
     with ExitStack() as stack:
         stack.enter_context(tc.manual_schedule())
         const = stack.enter_context(tc.tile_pool(name="const", bufs=1))
-        w_load = stack.enter_context(tc.tile_pool(name="w_load", bufs=COUT // (W_CHUNK * P)))
-        x_load = stack.enter_context(tc.tile_pool(name="x_load", bufs=T_BLOCKS))
+        w_load = stack.enter_context(tc.tile_pool(name="w_load", bufs=1))
         group = stack.enter_context(tc.tile_pool(name="group", bufs=2))
-        signed_pool = stack.enter_context(tc.tile_pool(name="signed", bufs=3))
-        act_pool = stack.enter_context(tc.tile_pool(name="act", bufs=AT_FLIP - AT_PRELU + 2))
-        waste_pool = stack.enter_context(tc.tile_pool(name="waste", bufs=3))
-        norm_pool = stack.enter_context(tc.tile_pool(name="norm", bufs=7))
+        signed_pool = stack.enter_context(tc.tile_pool(name="signed", bufs=4))
+        act_pool = stack.enter_context(tc.tile_pool(name="act", bufs=19))
+        waste_pool = stack.enter_context(tc.tile_pool(name="waste", bufs=2))
+        norm_pool = stack.enter_context(tc.tile_pool(name="norm", bufs=8))
         stat = stack.enter_context(tc.tile_pool(name="stat", bufs=3))
         psum_mx = stack.enter_context(tc.psum_pool(name="psum_mx", bufs=2))
-        psum_sum = stack.enter_context(tc.psum_pool(name="psum_sum", bufs=2))
-        psum_flip = stack.enter_context(tc.psum_pool(name="psum_flip", bufs=4))
+        psum_sum = stack.enter_context(tc.psum_pool(name="psum_sum", bufs=1))
+        psum_flip = stack.enter_context(tc.psum_pool(name="psum_flip", bufs=8 - 2 - 1))
+
+        x_rows = x[0].rearrange("(p k) f t -> p (k f) t", k=PACK)
+        alpha_bf = const.tile([P, 1], BF16)
+        bias_rows_bf = const.tile([P, P], BF16)
+        nc.vector.memset(bias_rows_bf[:], 0.0)
+        nc.sync.dma_start(out=alpha_bf[:], in_=qkv_alpha.partition_broadcast(P))
+        nc.sync.dma_start(out=bias_rows_bf[0:O_TILES, :], in_=qkv_b.rearrange("(a p) -> a p", p=P))
+        x_raw0 = const.tile([P, PACK * FREQ, P], BF16)
+        nc.sync.dma_start(out=x_raw0[:], in_=x_rows[:, :, 0:P])
+        w_raw = []
+
+        def load_w(i):
+            first = sum(W_GROUPS[:i])
+            raw = w_load.tile([P, W_GROUPS[i], CIN], BF16, name="w_raw%d" % i)
+            rows = qkv_w[first * P : (first + W_GROUPS[i]) * P, :]
+            nc.sync.dma_start(out=raw[:], in_=rows.rearrange("(a p) c -> p a c", p=P))
+            w_raw.append(raw)
+
+        load_w(0)
+        for i in range(1, len(W_GROUPS)):
+            load_w(i)
+        x_rest = const.tile([P, PACK * FREQ, T - P], BF16)
+        nc.sync.dma_start(out=x_rest[:], in_=x_rows[:, :, P:T])
+        gamma_bc = const.tile([P, ROW], BF16)
+        beta_bc = const.tile([P, ROW], BF16)
+        nc.sync.dma_start(out=gamma_bc[:], in_=qkv_gamma.rearrange("a o b f -> (a o b f)").partition_broadcast(P))
+        nc.sync.dma_start(out=beta_bc[:], in_=qkv_beta.rearrange("a o b f -> (a o b f)").partition_broadcast(P))
 
         ident = const.tile([P, P], F32)
         make_identity(nc, ident[:])
-
         one = const.tile([P, 1], F32)
         nc.vector.memset(one[:], 1.0)
         one_root = const.tile([P, 1], F32)
         nc.scalar.activation(out=one_root[:], in_=one[:], func=ACT.Sqrt)
-
         eps = const.tile([P, 1], F32)
         nc.vector.memset(eps[:], EPS)
 
-        alpha_bf = const.tile([P, 1], BF16)
-        nc.sync.dma_start(out=alpha_bf[:], in_=qkv_alpha.partition_broadcast(P))
-        bias_rows_bf = const.tile([P, P], BF16)
-        nc.vector.memset(bias_rows_bf[:], 0.0)
-        nc.sync.dma_start(out=bias_rows_bf[0:O_TILES, :], in_=qkv_b.rearrange("(a p) -> a p", p=P))
-
-        x_rows = x[0].rearrange("(p k) f t -> p (k f) t", k=PACK)
-        x_raw = []
-        w_raw = []
-
-        def load_x(tb):
-            raw = x_load.tile([P, PACK, BANK], BF16, name="x_raw")
-            nc.sync.dma_start(
-                out=raw[:].rearrange("p k (f t) -> p (k f) t", t=P),
-                in_=x_rows[:, :, tb * P : (tb + 1) * P],
-            )
-            x_raw.append(raw)
-
-        def load_w(chunk):
-            raw = w_load.tile([P, W_CHUNK, CIN], BF16, name="w_raw")
-            rows = qkv_w[chunk * W_CHUNK * P : (chunk + 1) * W_CHUNK * P, :]
-            nc.sync.dma_start(out=raw[:], in_=rows.rearrange("(a p) c -> p a c", p=P))
-            w_raw.append(raw)
-
-        gamma_bc = const.tile([P, ROW], BF16)
-        beta_bc = const.tile([P, ROW], BF16)
-        load_w(0)
-        load_x(0)
-        load_w(1)
-        load_w(2)
-        load_x(1)
-        load_x(2)
-        load_x(3)
-        nc.sync.dma_start(
-            out=gamma_bc[:], in_=qkv_gamma.rearrange("a o b f -> (a o b f)").partition_broadcast(P)
-        )
-        nc.sync.dma_start(
-            out=beta_bc[:], in_=qkv_beta.rearrange("a o b f -> (a o b f)").partition_broadcast(P)
-        )
+        def small_constants():
+            nc.vector.tensor_copy(out=alpha[:], in_=alpha_bf[:])
+            nc.vector.tensor_scalar(out=sign[:], in0=alpha[:], scalar1=1.0, scalar2=-2.0, op0=ALU.is_gt, op1=ALU.mult)
+            nc.vector.tensor_scalar_add(out=sign[:], in0=sign[:], scalar1=1.0)
+            nc.vector.tensor_copy(out=bias_rows[:], in_=bias_rows_bf[:])
+            bias_cols = psum_flip.tile([P, P], F32, tag="flip")
+            nc.tensor.transpose(bias_cols[:], bias_rows[:], ident[:])
+            nc.vector.tensor_scalar_mul(out=signed_bias[:], in0=bias_cols[:, 0:O_TILES], scalar1=sign[:, 0:1])
 
         alpha = const.tile([P, 1], F32)
-        nc.vector.tensor_copy(out=alpha[:], in_=alpha_bf[:])
         sign = const.tile([P, 1], F32)
-        nc.vector.tensor_scalar(
-            out=sign[:], in0=alpha[:], scalar1=1.0, scalar2=-2.0, op0=ALU.is_gt, op1=ALU.mult
-        )
-        nc.vector.tensor_scalar_add(out=sign[:], in0=sign[:], scalar1=1.0)
-
         bias_rows = const.tile([P, P], F32)
-        nc.vector.tensor_copy(out=bias_rows[:], in_=bias_rows_bf[:])
-        bias_cols = psum_flip.tile([P, P], F32, tag="flip")
-        nc.tensor.transpose(bias_cols[:], bias_rows[:], ident[:])
         signed_bias = const.tile([P, O_TILES], F32)
-        nc.vector.tensor_scalar_mul(
-            out=signed_bias[:], in0=bias_cols[:, 0:O_TILES], scalar1=sign[:, 0:1]
-        )
 
         w_codes = const.tile([P, COUT], U32, align_bytes=64)
         w_scales = const.tile([P, COUT], U8, align_bytes=64)
+        w_grouped = {}
 
-        def quantise_w(chunk, copy_out):
-            words = w_raw[chunk][:].bitcast(F32).rearrange("p a (q u) -> p a u q", u=2)
-            grouped = group.tile([P, W_CHUNK * P, PACK], BF16, align_bytes=64, name="w_grouped")
-            grouped_words = grouped[:].bitcast(F32)
-            for half in range(2):
-                flipped = psum_flip.tile([P, 2, 2, P], F32, tag="flip", name="w_flipped")
-                for a in range(2):
+        w_flipped = {}
+
+        def flip_w(i):
+            n = W_GROUPS[i]
+            w_flipped[i] = []
+            words = w_raw[i][:].bitcast(F32).rearrange("p a (q u) -> p a u q", u=2)
+            for a0 in range(0, n, 2):
+                m = min(2, n - a0)
+                flipped = psum_flip.tile([P, m, 2, P], F32, tag="flip", name="w_flipped")
+                for a in range(m):
                     for u in range(2):
-                        nc.tensor.transpose(flipped[:, a, u, :], words[:, 2 * half + a, u, :], ident[:])
-                dst = grouped_words[:, 2 * half * P : (2 * half + 2) * P, :]
-                copy_out(
-                    out=dst.rearrange("p (a o) u -> p a o u", a=2),
+                        nc.tensor.transpose(flipped[:, a, u, :], words[:, a0 + a, u, :], ident[:])
+                w_flipped[i].append((a0, m, flipped))
+
+        def copy_w(i, eng):
+            grouped = group.tile([P, 4 * P, PACK], BF16, align_bytes=64, name="w_grouped")
+            w_grouped[i] = grouped
+            grouped_words = grouped[:].bitcast(F32)
+            for a0, m, flipped in w_flipped[i]:
+                dst = grouped_words[:, a0 * P : (a0 + m) * P, :]
+                eng(
+                    out=dst.rearrange("p (a o) u -> p a o u", a=m),
                     in_=flipped[:].rearrange("p a u o -> p a o u"),
                 )
-            cols = slice(chunk * W_CHUNK * P, (chunk + 1) * W_CHUNK * P)
+
+        def quantise_w(i):
+            n = W_GROUPS[i]
+            first = sum(W_GROUPS[:i])
+            cols = slice(first * P, (first + n) * P)
             nc.vector.quantize_mx(
                 out=w_codes[:, cols].bitcast(FP8X4),
                 scales=w_scales[:, cols],
-                in_=grouped[:].rearrange("p o k -> p (o k)"),
+                in_=w_grouped[i][:, 0 : n * P, :].rearrange("p o k -> p (o k)"),
             )
 
         x_codes = const.tile([P, T_BLOCKS, BANK], U32, align_bytes=64)
         x_scales = const.tile([P, T_BLOCKS, BANK], U8, align_bytes=64)
+        x_grouped = {}
+
+        def group_x(tb, engs):
+            grouped = group.tile([P, BANK, PACK], BF16, align_bytes=64, name="x_grouped")
+            x_grouped[tb] = grouped
+            src = x_raw0[:] if tb == 0 else x_rest[:, :, (tb - 1) * P : tb * P]
+            src = src.rearrange("p (k f) t -> p k f t", k=PACK)
+            dst = grouped[:].rearrange("p (f t) k -> p f t k", f=FREQ)
+            n = FREQ // len(engs)
+            for j, eng in enumerate(engs):
+                for f in range(j * n, (j + 1) * n):
+                    eng(
+                        out=dst[:, f].rearrange("p (c i) k -> p c k i", i=4),
+                        in_=src[:, :, f].rearrange("p k (c i) -> p c k i", i=4),
+                    )
 
         def quantise_x(tb):
-            grouped = group.tile([P, BANK, PACK], BF16, align_bytes=64, name="x_grouped")
-            nc.vector.tensor_copy(
-                out=grouped[:].rearrange("p (c i) k -> p c k i", i=4),
-                in_=x_raw[tb][:].rearrange("p k (c i) -> p c k i", i=4),
-            )
             nc.vector.quantize_mx(
                 out=x_codes[:, tb, :].bitcast(FP8X4),
                 scales=x_scales[:, tb, :],
-                in_=grouped[:].rearrange("p n k -> p (n k)"),
+                in_=x_grouped[tb][:].rearrange("p n k -> p (n k)"),
             )
 
         products = {}
@@ -180,6 +184,7 @@ def tile_unified2dattentiononframe_pa_kernel(
         acts = {}
         flips = {}
         norms = {}
+        pairs = {}
         row_sums = {}
         neg_mean = {}
         square_sums = {}
@@ -189,16 +194,15 @@ def tile_unified2dattentiononframe_pa_kernel(
         def multiply(g):
             o_cols = slice((g % O_TILES) * P, (g % O_TILES + 1) * P)
             products[g] = psum_mx.tile([P, BANK], F32, name="product")
-            for repeat in range(PRODUCT_REPEATS):
-                nc.tensor.matmul_mx(
-                    out=products[g][:],
-                    lhsT=w_codes[:, o_cols].bitcast(FP8X4),
-                    lhsT_scale=w_scales[:, o_cols],
-                    rhs=x_codes[:, g // O_TILES, :].bitcast(FP8X4),
-                    rhs_scale=x_scales[:, g // O_TILES, :],
-                    start=True,
-                    stop=True,
-                )
+            nc.tensor.matmul_mx(
+                out=products[g][:],
+                lhsT=w_codes[:, o_cols].bitcast(FP8X4),
+                lhsT_scale=w_scales[:, o_cols],
+                rhs=x_codes[:, g // O_TILES, :].bitcast(FP8X4),
+                rhs_scale=x_scales[:, g // O_TILES, :],
+                start=True,
+                stop=True,
+            )
 
         def add_bias(g):
             signeds[g] = signed_pool.tile([P, BANK], F32, name="signed")
@@ -232,9 +236,10 @@ def tile_unified2dattentiononframe_pa_kernel(
 
         def mean_of_block(tb):
             waste = waste_pool.tile([P, P], BF16, name="waste_mean")
-            neg_mean[tb] = stat.tile([P, 1], F32, name="neg_mean")
+            pairs[tb] = stat.tile([P, 2], F32, name="pair")
+            neg_mean[tb] = pairs[tb][:, 0:1]
             nc.scalar.activation(
-                out=waste[:], in_=row_sums[tb][:], func=ACT.Copy, scale=-1.0 / ROW, accum_out=neg_mean[tb][:]
+                out=waste[:], in_=row_sums[tb][:], func=ACT.Copy, scale=-1.0 / ROW, accum_out=neg_mean[tb]
             )
             square_sums[tb] = stat.tile([P, O_TILES], F32, name="square_sums")
 
@@ -244,25 +249,24 @@ def tile_unified2dattentiononframe_pa_kernel(
                 nc.tensor.transpose(flips[g][:, f, :], acts[g][:, f * P : (f + 1) * P], ident[:])
 
         def square(g):
-            waste = waste_pool.tile([P, BANK], BF16)
+            waste = waste_pool.tile([P, BANK], BF16, name="waste_square")
             nc.scalar.activation(
                 out=waste[:],
                 in_=flips[g][:].rearrange("p f o -> p (f o)"),
                 func=ACT.Square,
-                bias=neg_mean[g // O_TILES][:, 0:1],
+                bias=neg_mean[g // O_TILES],
                 scale=1.0,
                 accum_out=square_sums[g // O_TILES][:, g % O_TILES : g % O_TILES + 1],
             )
 
         def gain(g):
-            if g % PIECE_TILES == 0:
-                norms[g // PIECE_TILES] = norm_pool.tile([P, PIECE_COLS], F32, name="norm")
+            norm_of(g)
             part = slice((g % PIECE_TILES) * BANK, (g % PIECE_TILES + 1) * BANK)
             gamma_part = gamma_bc[:, (g % O_TILES) * BANK : (g % O_TILES + 1) * BANK]
             nc.vector.scalar_tensor_tensor(
                 out=norms[g // PIECE_TILES][:, part].rearrange("p (o f) -> p o f", f=FREQ),
                 in0=flips[g][:].rearrange("p f o -> p o f"),
-                scalar=neg_mean[g // O_TILES][:, 0:1],
+                scalar=neg_mean[g // O_TILES],
                 in1=gamma_part.rearrange("p (o f) -> p o f", f=FREQ),
                 op0=ALU.add,
                 op1=ALU.mult,
@@ -276,65 +280,79 @@ def tile_unified2dattentiononframe_pa_kernel(
             )
             deviation = stat.tile([P, 1], F32)
             nc.scalar.activation(out=deviation[:], in_=variance[:], func=ACT.Sqrt, bias=eps[:, 0:1], scale=1.0)
-            signed_deviation[tb] = stat.tile([P, 1], F32, name="signed_deviation")
-            nc.scalar.activation(out=signed_deviation[tb][:], in_=deviation[:], func=ACT.Copy, scale=sign[:, 0:1])
+            signed_deviation[tb] = pairs[tb][:, 1:2]
+            nc.scalar.activation(out=signed_deviation[tb], in_=deviation[:], func=ACT.Copy, scale=sign[:, 0:1])
 
         def rstd_of_block(tb):
             signed_rstd[tb] = stat.tile([P, 1], F32, name="signed_rstd")
-            nc.vector.reciprocal(out=signed_rstd[tb][:], in_=signed_deviation[tb][:])
+            nc.vector.reciprocal(out=signed_rstd[tb][:], in_=signed_deviation[tb])
 
-        def scale_shift_store(piece):
+        def norm_of(g):
+            if g // PIECE_TILES not in norms:
+                norms[g // PIECE_TILES] = norm_pool.tile([P, PIECE_COLS], F32, name="norm")
+            return norms[g // PIECE_TILES]
+
+        def store(piece):
             tb = piece // (O_TILES // PIECE_TILES)
             s = piece % (O_TILES // PIECE_TILES)
-            norm = norms[piece]
-            nc.vector.scalar_tensor_tensor(
-                out=norm[:],
-                in0=norm[:],
-                scalar=signed_rstd[tb][:, 0:1],
-                in1=beta_bc[:, s * PIECE_COLS : (s + 1) * PIECE_COLS],
-                op0=ALU.mult,
-                op1=ALU.add,
-            )
-            split = norm[:].rearrange("p (h w d) -> p h w d", h=PIECE_HEADS, w=3)
+            split = norms[piece][:].rearrange("p (h w d) -> p h w d", h=PIECE_HEADS, w=3)
             for w, out_w in enumerate(outs):
                 rows = out_w[0, s * PIECE_HEADS : (s + 1) * PIECE_HEADS, tb * P : (tb + 1) * P, :]
                 nc.sync.dma_start(out=rows.rearrange("h t d -> t h d"), in_=split[:, :, w, :])
 
-        def is_tile(g):
-            return 0 <= g < TILES
+        def scale_shift(g):
+            norm = norms[g // PIECE_TILES]
+            part = slice((g % PIECE_TILES) * BANK, (g % PIECE_TILES + 1) * BANK)
+            nc.vector.scalar_tensor_tensor(
+                out=norm[:, part],
+                in0=norm[:, part],
+                scalar=signed_rstd[g // O_TILES][:, 0:1],
+                in1=beta_bc[:, (g % O_TILES) * BANK : (g % O_TILES + 1) * BANK],
+                op0=ALU.mult,
+                op1=ALU.add,
+            )
 
-        def ends_block(g):
-            return is_tile(g) and g % O_TILES == O_TILES - 1
 
-        def ends_piece(g):
-            return is_tile(g) and g % PIECE_TILES == PIECE_TILES - 1
+        jobs = []
 
-        quantise_w(0, nc.scalar.copy)
-        quantise_x(0)
-        for n in range(STEPS):
-            if is_tile(n - AT_FLIP):
-                flip(n - AT_FLIP)
-            if is_tile(n - AT_SUM):
-                add_to_row_sums(n - AT_SUM)
-            if is_tile(n):
-                multiply(n)
-            if is_tile(n - AT_BIAS):
-                add_bias(n - AT_BIAS)
-            if is_tile(n - AT_SQUARE):
-                square(n - AT_SQUARE)
-            if ends_block(n - AT_SQUARE):
-                deviation_of_block((n - AT_SQUARE) // O_TILES)
-            if ends_block(n - AT_MEAN):
-                mean_of_block((n - AT_MEAN) // O_TILES)
-            if is_tile(n - AT_PRELU):
-                prelu(n - AT_PRELU)
-            if is_tile(n - AT_GAIN):
-                gain(n - AT_GAIN)
-            if ends_block(n - AT_RSTD):
-                rstd_of_block((n - AT_RSTD) // O_TILES)
-            if ends_piece(n - AT_SHIFT):
-                scale_shift_store((n - AT_SHIFT) // PIECE_TILES)
-            if n == 0 or n == 2:
-                quantise_w(n // 2 + 1, nc.vector.tensor_copy)
-            if n == 4 or n == 6 or n == 8:
-                quantise_x(n // 2 - 1)
+        def at(step, rank, job, *args):
+            jobs.append((step, rank, len(jobs), job, args))
+
+        first = 0
+        for i, n in enumerate(W_GROUPS):
+            at(first - 3, 0, flip_w, i)
+            at(first - 2.5, 3.5, copy_w, i, nc.scalar.copy)
+            at(first - 1.5, 6.5, quantise_w, i)
+            first += n
+        at(-10, 0, small_constants)
+        at(-5, 0, group_x, 0, [nc.vector.tensor_copy, nc.scalar.copy])
+        at(-4, 0, quantise_x, 0)
+        for b in (1, 2, 3):
+            at(XPOS[b - 1], 8, group_x, b, XS(nc, b))
+            at(XPOS[b - 1] + 3, 9, quantise_x, b)
+        for g in range(TILES):
+            tb = g // O_TILES
+            late = g % O_TILES == O_TILES - 1
+            i = g % O_TILES
+            end = tb * O_TILES + O_TILES - 1
+            q = g // TG * TG + (TG - 1)
+            at(q, 3, multiply, g)
+            at(q + AT_BIAS + (g % TG) - TG + 1, 4, add_bias, g)
+            at(g + AT_PRELU, 7, prelu, g)
+            at(q + AT_SUM, 2, add_to_row_sums, g)
+            at(q + AT_FLIP, 1, flip, g)
+            at(q + AT_SQUARE + (g % TG) - TG + 1, 5, square, g)
+            at(g + AT_GAIN, 7.5, gain, g)
+            last = end + AT_RSTD + AT_SHIFT + i * 1
+            at(last, 7.7, scale_shift, g)
+            if g % PIECE_TILES == 0:
+                piece_end = 0
+            piece_end = max(piece_end, last)
+            if g % PIECE_TILES == PIECE_TILES - 1:
+                at(piece_end, 9, store, g // PIECE_TILES)
+            if late:
+                at(q + AT_MEAN, 4.5, mean_of_block, tb)
+                at(g + AT_SQUARE, 5.5, deviation_of_block, tb)
+                at(g + AT_RSTD, 6.5, rstd_of_block, tb)
+        for step, rank, index, job, args in sorted(jobs, key=lambda j: j[:3]):
+            job(*args)

@@ -35,14 +35,13 @@ AT_BIAS = 1
 AT_PRELU = 3
 AT_SUM = 5
 AT_MEAN = 6
-AT_FLIP = O_TILES + AT_MEAN - 1 + 0
-AT_SQUARE = AT_FLIP + 1
-AT_GAIN = AT_FLIP + 2
-AT_RSTD = AT_SQUARE + 2
-TG = 1
-AT_SHIFT = 1
-XS = lambda nc, b: [nc.scalar.copy, nc.vector.tensor_copy]
-XPOS = (7,12,17)
+TG = 2
+KIND = lambda g: "2VVS"[g % 4] if g >= 24 else "V"
+LAST = T_BLOCKS - 1 if 0 else T_BLOCKS
+EARLY = 0
+TWICE = 3
+XS = lambda nc, b: [nc.scalar.copy, nc.vector.tensor_copy] if b == 1 else [nc.vector.tensor_copy]
+XPOS = (7,17,23)
 
 
 def tile_unified2dattentiononframe_pa_kernel(
@@ -57,22 +56,19 @@ def tile_unified2dattentiononframe_pa_kernel(
         w_load = stack.enter_context(tc.tile_pool(name="w_load", bufs=1))
         group = stack.enter_context(tc.tile_pool(name="group", bufs=2))
         signed_pool = stack.enter_context(tc.tile_pool(name="signed", bufs=4))
-        act_pool = stack.enter_context(tc.tile_pool(name="act", bufs=19))
+        bend_pool = stack.enter_context(tc.tile_pool(name="bend", bufs=8))
+        act_pool = stack.enter_context(tc.tile_pool(name="act", bufs=20))
         waste_pool = stack.enter_context(tc.tile_pool(name="waste", bufs=2))
         norm_pool = stack.enter_context(tc.tile_pool(name="norm", bufs=8))
         stat = stack.enter_context(tc.tile_pool(name="stat", bufs=3))
-        psum_mx = stack.enter_context(tc.psum_pool(name="psum_mx", bufs=2))
+        psum_mx = stack.enter_context(tc.psum_pool(name="psum_mx", bufs=3))
         psum_sum = stack.enter_context(tc.psum_pool(name="psum_sum", bufs=1))
-        psum_flip = stack.enter_context(tc.psum_pool(name="psum_flip", bufs=8 - 2 - 1))
+        psum_flip = stack.enter_context(tc.psum_pool(name="psum_flip", bufs=8 - 3 - 1))
 
         x_rows = x[0].rearrange("(p k) f t -> p (k f) t", k=PACK)
         alpha_bf = const.tile([P, 1], BF16)
         bias_rows_bf = const.tile([P, P], BF16)
         nc.vector.memset(bias_rows_bf[:], 0.0)
-        nc.sync.dma_start(out=alpha_bf[:], in_=qkv_alpha.partition_broadcast(P))
-        nc.sync.dma_start(out=bias_rows_bf[0:O_TILES, :], in_=qkv_b.rearrange("(a p) -> a p", p=P))
-        x_raw0 = const.tile([P, PACK * FREQ, P], BF16)
-        nc.sync.dma_start(out=x_raw0[:], in_=x_rows[:, :, 0:P])
         w_raw = []
 
         def load_w(i):
@@ -83,8 +79,21 @@ def tile_unified2dattentiononframe_pa_kernel(
             w_raw.append(raw)
 
         load_w(0)
-        for i in range(1, len(W_GROUPS)):
+        x_raw0 = []
+        for half in range(2):
+            raw = const.tile([P, PACK, 2, P], BF16, name="x_raw0_%d" % half)
+            nc.sync.dma_start(
+                out=raw[:],
+                in_=x[0].rearrange("(p k) f t -> p k f t", k=PACK)[:, :, 2 * half : 2 * half + 2, 0:P],
+            )
+            x_raw0.append(raw)
+        nc.sync.dma_start(out=alpha_bf[:], in_=qkv_alpha.partition_broadcast(P))
+        load_w(1)
+        load_w(2)
+        nc.sync.dma_start(out=bias_rows_bf[0:O_TILES, :], in_=qkv_b.rearrange("(a p) -> a p", p=P))
+        for i in range(3, len(W_GROUPS)):
             load_w(i)
+
         x_rest = const.tile([P, PACK * FREQ, T - P], BF16)
         nc.sync.dma_start(out=x_rest[:], in_=x_rows[:, :, P:T])
         gamma_bc = const.tile([P, ROW], BF16)
@@ -101,17 +110,27 @@ def tile_unified2dattentiononframe_pa_kernel(
         eps = const.tile([P, 1], F32)
         nc.vector.memset(eps[:], EPS)
 
-        def small_constants():
-            nc.vector.tensor_copy(out=alpha[:], in_=alpha_bf[:])
-            nc.vector.tensor_scalar(out=sign[:], in0=alpha[:], scalar1=1.0, scalar2=-2.0, op0=ALU.is_gt, op1=ALU.mult)
-            nc.vector.tensor_scalar_add(out=sign[:], in0=sign[:], scalar1=1.0)
-            nc.vector.tensor_copy(out=bias_rows[:], in_=bias_rows_bf[:])
+        def slope_constants():
+            nc.gpsimd.tensor_copy(out=alpha[:], in_=alpha_bf[:])
+            nc.gpsimd.tensor_scalar(out=sign[:], in0=alpha[:], scalar1=1.0, scalar2=-2.0, op0=ALU.is_gt, op1=ALU.mult)
+            nc.gpsimd.tensor_scalar(out=sign[:], in0=sign[:], scalar1=1.0, scalar2=1.0, op0=ALU.add, op1=ALU.mult)
+            nc.gpsimd.tensor_scalar(out=bend[:], in0=alpha[:], scalar1=-1.0, scalar2=1.0, op0=ALU.add, op1=ALU.mult)
+            nc.gpsimd.tensor_tensor(out=signed_bend[:], in0=bend[:], in1=sign[:], op=ALU.mult)
+            nc.gpsimd.tensor_copy(out=bias_rows[:], in_=bias_rows_bf[:])
+
+        def bias_constants():
             bias_cols = psum_flip.tile([P, P], F32, tag="flip")
             nc.tensor.transpose(bias_cols[:], bias_rows[:], ident[:])
-            nc.vector.tensor_scalar_mul(out=signed_bias[:], in0=bias_cols[:, 0:O_TILES], scalar1=sign[:, 0:1])
+            nc.scalar.activation(out=signed_bias[:], in_=bias_cols[:, 0:O_TILES], func=ACT.Copy, scale=sign[:, 0:1])
+            nc.gpsimd.tensor_scalar(
+                out=bend_bias[:], in0=signed_bias[:], scalar1=bend[:, 0:1], scalar2=0.0, op0=ALU.mult, op1=ALU.add
+            )
 
         alpha = const.tile([P, 1], F32)
         sign = const.tile([P, 1], F32)
+        bend = const.tile([P, 1], F32)
+        signed_bend = const.tile([P, 1], F32)
+        bend_bias = const.tile([P, O_TILES], F32)
         bias_rows = const.tile([P, P], F32)
         signed_bias = const.tile([P, O_TILES], F32)
 
@@ -161,16 +180,17 @@ def tile_unified2dattentiononframe_pa_kernel(
         def group_x(tb, engs):
             grouped = group.tile([P, BANK, PACK], BF16, align_bytes=64, name="x_grouped")
             x_grouped[tb] = grouped
-            src = x_raw0[:] if tb == 0 else x_rest[:, :, (tb - 1) * P : tb * P]
-            src = src.rearrange("p (k f) t -> p k f t", k=PACK)
             dst = grouped[:].rearrange("p (f t) k -> p f t k", f=FREQ)
             n = FREQ // len(engs)
-            for j, eng in enumerate(engs):
-                for f in range(j * n, (j + 1) * n):
-                    eng(
-                        out=dst[:, f].rearrange("p (c i) k -> p c k i", i=4),
-                        in_=src[:, :, f].rearrange("p k (c i) -> p c k i", i=4),
-                    )
+            for f in range(FREQ):
+                if tb == 0:
+                    src = x_raw0[f // 2][:, :, f % 2, :]
+                else:
+                    src = x_rest[:].rearrange("p (k f) t -> p k f t", k=PACK)[:, :, f, (tb - 1) * P : tb * P]
+                engs[f // n](
+                    out=dst[:, f].rearrange("p (c i) k -> p c k i", i=4),
+                    in_=src.rearrange("p k (c i) -> p c k i", i=4),
+                )
 
         def quantise_x(tb):
             nc.vector.quantize_mx(
@@ -186,6 +206,21 @@ def tile_unified2dattentiononframe_pa_kernel(
         norms = {}
         pairs = {}
         row_sums = {}
+        early_flips = {}
+        early_sums = const.tile([P, O_TILES], F32)
+        neg_early = const.tile([P, 1], F32)
+
+        def sum_group(g):
+            tb = g // O_TILES
+            first = tb * O_TILES
+            last = first + O_TILES - 1
+            if tb == LAST:
+                if g < first + EARLY:
+                    last = first + EARLY - 1
+                else:
+                    first = first + EARLY
+            return first, last
+
         neg_mean = {}
         square_sums = {}
         signed_deviation = {}
@@ -204,8 +239,13 @@ def tile_unified2dattentiononframe_pa_kernel(
                 stop=True,
             )
 
+        parts = {}
+
         def add_bias(g):
-            signeds[g] = signed_pool.tile([P, BANK], F32, name="signed")
+            if KIND(g) == "V":
+                signeds[g] = signed_pool.tile([P, BANK], F32, name="signed")
+            else:
+                signeds[g] = act_pool.tile([P, BANK], F32, name="act")
             nc.scalar.activation(
                 out=signeds[g][:],
                 in_=products[g][:],
@@ -214,39 +254,93 @@ def tile_unified2dattentiononframe_pa_kernel(
                 scale=sign[:, 0:1],
             )
 
+        def bend_s(g):
+            bends = bend_pool.tile([P, BANK], F32, name="bends")
+            nc.scalar.activation(out=bends[:], in_=products[g][:], func=ACT.Relu, bias=bend_bias[:, g % O_TILES : g % O_TILES + 1], scale=signed_bend[:, 0:1])
+            parts[g] = [signeds[g], bends]
+
+        def bend_v(g):
+            bends = bend_pool.tile([P, BANK], F32, name="bends")
+            nc.vector.tensor_scalar(out=bends[:], in0=signeds[g][:], scalar1=bend[:, 0:1], scalar2=0.0, op0=ALU.mult, op1=ALU.max)
+            parts[g] = [signeds[g], bends]
+
         def prelu(g):
             acts[g] = act_pool.tile([P, BANK], F32, name="act")
             nc.vector.scalar_tensor_tensor(
                 out=acts[g][:], in0=signeds[g][:], scalar=alpha[:, 0:1], in1=signeds[g][:], op0=ALU.mult, op1=ALU.max
             )
+            parts[g] = [acts[g]]
 
         def add_to_row_sums(g):
-            tb = g // O_TILES
-            if g % O_TILES == 0:
-                row_sums[tb] = psum_sum.tile([P, P], F32, name="row_sums")
-            for f in range(FREQ):
-                nc.tensor.matmul(
-                    out=row_sums[tb][:],
-                    lhsT=acts[g][:, f * P : (f + 1) * P],
-                    rhs=ident[:],
-                    is_transpose=True,
-                    start=(g % O_TILES == 0 and f == 0),
-                    stop=(g % O_TILES == O_TILES - 1 and f == FREQ - 1),
-                )
+            first, last = sum_group(g)
+            if g == first:
+                row_sums[g] = psum_sum.tile([P, P], F32, name="row_sums")
+            for j, part in enumerate(parts[g]):
+                for f in range(FREQ):
+                    nc.tensor.matmul(
+                        out=row_sums[first][:],
+                        lhsT=part[:, f * P : (f + 1) * P],
+                        rhs=ident[:],
+                        is_transpose=True,
+                        start=(g == first and j == 0 and f == 0),
+                        stop=(g == last and j == len(parts[g]) - 1 and f == FREQ - 1),
+                    )
 
         def mean_of_block(tb):
+            square_sums[tb] = stat.tile([P, O_TILES + 1], F32, name="square_sums")
+            mean_tile = stat.tile([P, 1], F32, name="neg_mean")
+            neg_mean[tb] = mean_tile[:, 0:1]
             waste = waste_pool.tile([P, P], BF16, name="waste_mean")
-            pairs[tb] = stat.tile([P, 2], F32, name="pair")
-            neg_mean[tb] = pairs[tb][:, 0:1]
+            if tb != LAST:
+                nc.scalar.activation(
+                    out=waste[:], in_=row_sums[tb * O_TILES][:], func=ACT.Copy, scale=-1.0 / ROW, accum_out=neg_mean[tb]
+                )
+            else:
+                rest = stat.tile([P, 1], F32, name="neg_rest")
+                nc.scalar.activation(
+                    out=waste[:], in_=row_sums[tb * O_TILES + EARLY][:], func=ACT.Copy, scale=-1.0 / ROW, accum_out=rest[:]
+                )
+                nc.scalar.activation(
+                    out=neg_mean[tb], in_=neg_early[:], func=ACT.Identity, bias=rest[:, 0:1], scale=EARLY / O_TILES
+                )
+                gap = stat.tile([P, 1], F32, name="gap")
+                nc.scalar.activation(out=gap[:], in_=neg_early[:], func=ACT.Square, bias=neg_mean[tb], scale=-1.0)
+                nc.scalar.activation(out=square_sums[tb][:, O_TILES : O_TILES + 1], in_=gap[:], func=ACT.Copy, scale=float(EARLY * BANK))
+
+        def early_mean():
+            waste = waste_pool.tile([P, P], BF16, name="waste_mean")
             nc.scalar.activation(
-                out=waste[:], in_=row_sums[tb][:], func=ACT.Copy, scale=-1.0 / ROW, accum_out=neg_mean[tb]
+                out=waste[:], in_=row_sums[LAST * O_TILES][:], func=ACT.Copy, scale=-1.0 / (EARLY * BANK), accum_out=neg_early[:]
             )
-            square_sums[tb] = stat.tile([P, O_TILES], F32, name="square_sums")
 
         def flip(g):
             flips[g] = psum_flip.tile([P, FREQ, P], F32, tag="flip", name="flipped")
             for f in range(FREQ):
-                nc.tensor.transpose(flips[g][:, f, :], acts[g][:, f * P : (f + 1) * P], ident[:])
+                for j, part in enumerate(parts[g]):
+                    nc.tensor.matmul(
+                        out=flips[g][:, f, :],
+                        lhsT=part[:, f * P : (f + 1) * P],
+                        rhs=ident[:],
+                        is_transpose=True,
+                        start=j == 0,
+                        stop=j == len(parts[g]) - 1,
+                    )
+
+        def early_flip(g):
+            early_flips[g] = psum_flip.tile([P, FREQ, P], F32, tag="flip", name="flipped")
+            for f in range(FREQ):
+                nc.tensor.transpose(early_flips[g][:, f, :], acts[g][:, f * P : (f + 1) * P], ident[:])
+
+        def early_square(g):
+            waste = waste_pool.tile([P, BANK], BF16, name="waste_square")
+            nc.scalar.activation(
+                out=waste[:],
+                in_=early_flips[g][:].rearrange("p f o -> p (f o)"),
+                func=ACT.Square,
+                bias=neg_early[:, 0:1],
+                scale=1.0,
+                accum_out=early_sums[:, g % O_TILES : g % O_TILES + 1],
+            )
 
         def square(g):
             waste = waste_pool.tile([P, BANK], BF16, name="waste_square")
@@ -273,14 +367,19 @@ def tile_unified2dattentiononframe_pa_kernel(
             )
 
         def deviation_of_block(tb):
-            waste = waste_pool.tile([P, O_TILES], BF16, name="waste_variance")
+            columns = O_TILES
+            if tb == LAST:
+                columns = O_TILES + 1
+                nc.scalar.activation(out=square_sums[tb][:, 0:EARLY], in_=early_sums[:, 0:EARLY], func=ACT.Copy, scale=1.0)
+            waste = waste_pool.tile([P, O_TILES + 1], BF16, name="waste_variance")
             variance = stat.tile([P, 1], F32)
             nc.scalar.activation(
-                out=waste[:], in_=square_sums[tb][:], func=ACT.Copy, scale=1.0 / ROW, accum_out=variance[:]
+                out=waste[:, 0:columns], in_=square_sums[tb][:, 0:columns], func=ACT.Copy, scale=1.0 / ROW, accum_out=variance[:]
             )
             deviation = stat.tile([P, 1], F32)
             nc.scalar.activation(out=deviation[:], in_=variance[:], func=ACT.Sqrt, bias=eps[:, 0:1], scale=1.0)
-            signed_deviation[tb] = pairs[tb][:, 1:2]
+            sdev = stat.tile([P, 1], F32, name="signed_deviation")
+            signed_deviation[tb] = sdev[:, 0:1]
             nc.scalar.activation(out=signed_deviation[tb], in_=deviation[:], func=ACT.Copy, scale=sign[:, 0:1])
 
         def rstd_of_block(tb):
@@ -291,6 +390,16 @@ def tile_unified2dattentiononframe_pa_kernel(
             if g // PIECE_TILES not in norms:
                 norms[g // PIECE_TILES] = norm_pool.tile([P, PIECE_COLS], F32, name="norm")
             return norms[g // PIECE_TILES]
+
+        def store_tile(g):
+            tb = g // O_TILES
+            for half in range(2):
+                segment = 2 * (g % O_TILES) + half
+                column = (2 * (g % PIECE_TILES) + half) * HEAD_DIM
+                nc.sync.dma_start(
+                    out=outs[segment % 3][0, segment // 3, tb * P : (tb + 1) * P, :],
+                    in_=norms[g // PIECE_TILES][:, column : column + HEAD_DIM],
+                )
 
         def store(piece):
             tb = piece // (O_TILES // PIECE_TILES)
@@ -320,11 +429,12 @@ def tile_unified2dattentiononframe_pa_kernel(
 
         first = 0
         for i, n in enumerate(W_GROUPS):
-            at(first - 3, 0, flip_w, i)
-            at(first - 2.5, 3.5, copy_w, i, nc.scalar.copy)
-            at(first - 1.5, 6.5, quantise_w, i)
+            at(first - 2, 0, flip_w, i)
+            at(first - 1.5, 3.5, copy_w, i, nc.scalar.copy if i % 2 == 0 else nc.vector.tensor_copy)
+            at(first - 0.5, 6.5, quantise_w, i)
             first += n
-        at(-10, 0, small_constants)
+        at(-10, 0, slope_constants)
+        at(1, 3.5, bias_constants)
         at(-5, 0, group_x, 0, [nc.vector.tensor_copy, nc.scalar.copy])
         at(-4, 0, quantise_x, 0)
         for b in (1, 2, 3):
@@ -332,27 +442,52 @@ def tile_unified2dattentiononframe_pa_kernel(
             at(XPOS[b - 1] + 3, 9, quantise_x, b)
         for g in range(TILES):
             tb = g // O_TILES
-            late = g % O_TILES == O_TILES - 1
             i = g % O_TILES
-            end = tb * O_TILES + O_TILES - 1
             q = g // TG * TG + (TG - 1)
+            base = tb * O_TILES + O_TILES - 1 + AT_MEAN
+            j = i if tb != LAST else (i - EARLY) % O_TILES
+            squares = O_TILES if tb != LAST else O_TILES - EARLY
+            pace = ((.75,.75,.75,1))[tb]
+            turn = base + 1 + (j // TG) * TG * pace
+            ready = base + 1 + (squares - TG) * pace + 1
             at(q, 3, multiply, g)
             at(q + AT_BIAS + (g % TG) - TG + 1, 4, add_bias, g)
-            at(g + AT_PRELU, 7, prelu, g)
+            if KIND(g) == "S":
+                at(q + AT_BIAS + (g % TG) - TG + 1, 4.1, bend_s, g)
+            else:
+                at(g + AT_PRELU, 7, prelu if KIND(g) == "V" else bend_v, g)
             at(q + AT_SUM, 2, add_to_row_sums, g)
-            at(q + AT_FLIP, 1, flip, g)
-            at(q + AT_SQUARE + (g % TG) - TG + 1, 5, square, g)
-            at(g + AT_GAIN, 7.5, gain, g)
-            last = end + AT_RSTD + AT_SHIFT + i * 1
+            if tb == TWICE:
+                turn = base + 1 + (i // TG) * TG * 0.75
+                ready = base + 1 + (O_TILES - TG) * 0.75 + 1
+                at(turn, 1, flip, g)
+                at(turn + (g % TG) * 0.75, 5, square, g)
+                turn = base + 6 + (i // TG) * TG * 1
+                pace = 1
+                at(turn, 1, flip, g)
+            elif j < squares:
+                at(turn, 1, flip, g)
+                at(turn + (g % TG) * pace, 5, square, g)
+            else:
+                at(turn, 1, flip, g)
+                early = TILES + 0 + (i // TG) * TG
+                at(early, 1.5, early_flip, g)
+                at(early + g % TG, 5.2, early_square, g)
+            at(turn + (g % TG) * pace + 0, 7.5, gain, g)
+            last = ready + (1 if tb != TWICE else 1) + 1 + j * ((1, 1, 1, 1))[tb]
             at(last, 7.7, scale_shift, g)
             if g % PIECE_TILES == 0:
                 piece_end = 0
             piece_end = max(piece_end, last)
-            if g % PIECE_TILES == PIECE_TILES - 1:
+            if (tb, i // PIECE_TILES) in ((3,0),(3,1),(3,2),(3,3)):
+                at(last, 9, store_tile, g)
+            elif g % PIECE_TILES == PIECE_TILES - 1:
                 at(piece_end, 9, store, g // PIECE_TILES)
-            if late:
-                at(q + AT_MEAN, 4.5, mean_of_block, tb)
-                at(g + AT_SQUARE, 5.5, deviation_of_block, tb)
-                at(g + AT_RSTD, 6.5, rstd_of_block, tb)
+            if i == O_TILES - 1:
+                at(base, 4.5, mean_of_block, tb)
+                at(ready, 5.5, deviation_of_block, tb)
+                at(ready + (1 if tb != TWICE else 1), 6.5, rstd_of_block, tb)
+        if EARLY:
+            at(LAST * O_TILES + EARLY - 1 + AT_MEAN, 4.5, early_mean)
         for step, rank, index, job, args in sorted(jobs, key=lambda j: j[:3]):
             job(*args)

@@ -31,15 +31,33 @@ TILES = T_BLOCKS * O_TILES
 FLOPS = 2 * COUT * CIN * FREQ * T
 
 W_GROUPS = (1,1,2,2,2,2,2)
-AT_BIAS = 1
+AT_BIAS = 2
 AT_PRELU = 3
 AT_SUM = 5
-AT_MEAN = 6
+AT_MEAN = 5
 TG = 2
-KIND = lambda g: "2VVS"[g % 4] if g >= 24 else "V"
-LAST = T_BLOCKS - 1 if 0 else T_BLOCKS
-EARLY = 0
-TWICE = 3
+NB = 8
+BB = 14
+AB = 22
+AT_P = (3, 3, 3, 3)
+KB = ("V", "V", "2VS", "2VS")
+KIND = lambda g: KB[g // O_TILES][g % len(KB[g // O_TILES])]
+FOLD2 = 12
+FOLD3 = 0
+PB = (0.75, 0.75, 0.75, 0.5)
+SH = (1, 1, 1, 1)
+SHP = (1, 1, 1, 1)
+GP_AT = 1
+PRE = 5
+MR = 2
+GP_PACE = 1
+GP_ENG = "VVS"
+
+
+def fold_tile(g):
+    return (g // O_TILES == 3 and g % O_TILES >= FOLD3) or (g // O_TILES == 2 and g % O_TILES >= FOLD2)
+
+
 XS = lambda nc, b: [nc.scalar.copy, nc.vector.tensor_copy] if b == 1 else [nc.vector.tensor_copy]
 XPOS = (7,17,23)
 
@@ -51,15 +69,15 @@ def tile_unified2dattentiononframe_pa_kernel(
     outs = (out_0, out_1, out_2)
 
     with ExitStack() as stack:
-        stack.enter_context(tc.manual_schedule())
+        stack.enter_context(tc.manual_schedule(engines={mybir.EngineType.PE}))
         const = stack.enter_context(tc.tile_pool(name="const", bufs=1))
         w_load = stack.enter_context(tc.tile_pool(name="w_load", bufs=1))
         group = stack.enter_context(tc.tile_pool(name="group", bufs=2))
         signed_pool = stack.enter_context(tc.tile_pool(name="signed", bufs=4))
-        bend_pool = stack.enter_context(tc.tile_pool(name="bend", bufs=8))
-        act_pool = stack.enter_context(tc.tile_pool(name="act", bufs=20))
+        bend_pool = stack.enter_context(tc.tile_pool(name="bend", bufs=BB))
+        act_pool = stack.enter_context(tc.tile_pool(name="act", bufs=AB))
         waste_pool = stack.enter_context(tc.tile_pool(name="waste", bufs=2))
-        norm_pool = stack.enter_context(tc.tile_pool(name="norm", bufs=8))
+        norm_pool = stack.enter_context(tc.tile_pool(name="norm", bufs=NB))
         stat = stack.enter_context(tc.tile_pool(name="stat", bufs=3))
         psum_mx = stack.enter_context(tc.psum_pool(name="psum_mx", bufs=3))
         psum_sum = stack.enter_context(tc.psum_pool(name="psum_sum", bufs=1))
@@ -98,8 +116,16 @@ def tile_unified2dattentiononframe_pa_kernel(
         nc.sync.dma_start(out=x_rest[:], in_=x_rows[:, :, P:T])
         gamma_bc = const.tile([P, ROW], BF16)
         beta_bc = const.tile([P, ROW], BF16)
+        gamma_cols_bf = const.tile([P, O_TILES, FREQ], BF16)
+        gamma_cols = const.tile([P, O_TILES, FREQ], F32)
+        stat_rows = const.tile([P, P], BF16)
+        nc.gpsimd.memset(stat_rows[:], 0.0)
+        ident_bf = const.tile([P, P], BF16)
+        make_identity(nc, ident_bf[:])
         nc.sync.dma_start(out=gamma_bc[:], in_=qkv_gamma.rearrange("a o b f -> (a o b f)").partition_broadcast(P))
         nc.sync.dma_start(out=beta_bc[:], in_=qkv_beta.rearrange("a o b f -> (a o b f)").partition_broadcast(P))
+
+        nc.sync.dma_start(out=gamma_cols_bf[:], in_=qkv_gamma.rearrange("a (i p) b f -> p i (a b f)", p=P))
 
         ident = const.tile([P, P], F32)
         make_identity(nc, ident[:])
@@ -153,7 +179,7 @@ def tile_unified2dattentiononframe_pa_kernel(
                 w_flipped[i].append((a0, m, flipped))
 
         def copy_w(i, eng):
-            grouped = group.tile([P, 4 * P, PACK], BF16, align_bytes=64, name="w_grouped")
+            grouped = group.tile([P, 2 * P, PACK], BF16, align_bytes=64, name="w_grouped")
             w_grouped[i] = grouped
             grouped_words = grouped[:].bitcast(F32)
             for a0, m, flipped in w_flipped[i]:
@@ -206,19 +232,11 @@ def tile_unified2dattentiononframe_pa_kernel(
         norms = {}
         pairs = {}
         row_sums = {}
-        early_flips = {}
-        early_sums = const.tile([P, O_TILES], F32)
-        neg_early = const.tile([P, 1], F32)
 
         def sum_group(g):
             tb = g // O_TILES
             first = tb * O_TILES
             last = first + O_TILES - 1
-            if tb == LAST:
-                if g < first + EARLY:
-                    last = first + EARLY - 1
-                else:
-                    first = first + EARLY
             return first, last
 
         neg_mean = {}
@@ -228,7 +246,7 @@ def tile_unified2dattentiononframe_pa_kernel(
 
         def multiply(g):
             o_cols = slice((g % O_TILES) * P, (g % O_TILES + 1) * P)
-            products[g] = psum_mx.tile([P, BANK], F32, name="product")
+            products[g] = psum_mx.tile([P, BANK], F32, tag="product", name="product")
             nc.tensor.matmul_mx(
                 out=products[g][:],
                 lhsT=w_codes[:, o_cols].bitcast(FP8X4),
@@ -291,26 +309,8 @@ def tile_unified2dattentiononframe_pa_kernel(
             mean_tile = stat.tile([P, 1], F32, name="neg_mean")
             neg_mean[tb] = mean_tile[:, 0:1]
             waste = waste_pool.tile([P, P], BF16, name="waste_mean")
-            if tb != LAST:
-                nc.scalar.activation(
-                    out=waste[:], in_=row_sums[tb * O_TILES][:], func=ACT.Copy, scale=-1.0 / ROW, accum_out=neg_mean[tb]
-                )
-            else:
-                rest = stat.tile([P, 1], F32, name="neg_rest")
-                nc.scalar.activation(
-                    out=waste[:], in_=row_sums[tb * O_TILES + EARLY][:], func=ACT.Copy, scale=-1.0 / ROW, accum_out=rest[:]
-                )
-                nc.scalar.activation(
-                    out=neg_mean[tb], in_=neg_early[:], func=ACT.Identity, bias=rest[:, 0:1], scale=EARLY / O_TILES
-                )
-                gap = stat.tile([P, 1], F32, name="gap")
-                nc.scalar.activation(out=gap[:], in_=neg_early[:], func=ACT.Square, bias=neg_mean[tb], scale=-1.0)
-                nc.scalar.activation(out=square_sums[tb][:, O_TILES : O_TILES + 1], in_=gap[:], func=ACT.Copy, scale=float(EARLY * BANK))
-
-        def early_mean():
-            waste = waste_pool.tile([P, P], BF16, name="waste_mean")
             nc.scalar.activation(
-                out=waste[:], in_=row_sums[LAST * O_TILES][:], func=ACT.Copy, scale=-1.0 / (EARLY * BANK), accum_out=neg_early[:]
+                out=waste[:], in_=row_sums[tb * O_TILES][:], func=ACT.Copy, scale=-1.0 / ROW, accum_out=neg_mean[tb]
             )
 
         def flip(g):
@@ -325,22 +325,6 @@ def tile_unified2dattentiononframe_pa_kernel(
                         start=j == 0,
                         stop=j == len(parts[g]) - 1,
                     )
-
-        def early_flip(g):
-            early_flips[g] = psum_flip.tile([P, FREQ, P], F32, tag="flip", name="flipped")
-            for f in range(FREQ):
-                nc.tensor.transpose(early_flips[g][:, f, :], acts[g][:, f * P : (f + 1) * P], ident[:])
-
-        def early_square(g):
-            waste = waste_pool.tile([P, BANK], BF16, name="waste_square")
-            nc.scalar.activation(
-                out=waste[:],
-                in_=early_flips[g][:].rearrange("p f o -> p (f o)"),
-                func=ACT.Square,
-                bias=neg_early[:, 0:1],
-                scale=1.0,
-                accum_out=early_sums[:, g % O_TILES : g % O_TILES + 1],
-            )
 
         def square(g):
             waste = waste_pool.tile([P, BANK], BF16, name="waste_square")
@@ -368,9 +352,6 @@ def tile_unified2dattentiononframe_pa_kernel(
 
         def deviation_of_block(tb):
             columns = O_TILES
-            if tb == LAST:
-                columns = O_TILES + 1
-                nc.scalar.activation(out=square_sums[tb][:, 0:EARLY], in_=early_sums[:, 0:EARLY], func=ACT.Copy, scale=1.0)
             waste = waste_pool.tile([P, O_TILES + 1], BF16, name="waste_variance")
             variance = stat.tile([P, 1], F32)
             nc.scalar.activation(
@@ -422,6 +403,71 @@ def tile_unified2dattentiononframe_pa_kernel(
             )
 
 
+        scaled = {}
+
+        def scale_rows(g, eng):
+            assert g in flips
+            scaled[g] = []
+            for whole in parts[g]:
+                copy = whole
+                scaled[g].append(copy)
+                for f in range(FREQ):
+                    part = slice(f * P, (f + 1) * P)
+                    col = gamma_cols[:, g % O_TILES, f : f + 1]
+                    if eng == "V":
+                        nc.vector.tensor_scalar(out=copy[:, part], in0=whole[:, part], scalar1=col, scalar2=0.0, op0=ALU.mult, op1=ALU.add)
+                    else:
+                        nc.scalar.activation(out=copy[:, part], in_=whole[:, part], func=ACT.Copy, scale=col)
+
+        mean_lhs = {}
+
+        def mean_rows(tb):
+            rest = stat.tile([P, 1], F32, name="rest")
+            hi, mid, lo = (stat_rows[:, 2 * i : 2 * i + 1] for i in range(3))
+            nc.scalar.activation(out=hi, in_=neg_mean[tb], func=ACT.Copy)
+            nc.scalar.activation(out=rest[:], in_=hi, func=ACT.Identity, bias=neg_mean[tb], scale=-1.0)
+            nc.scalar.activation(out=mid, in_=rest[:], func=ACT.Copy)
+            nc.scalar.activation(out=lo, in_=mid, func=ACT.Identity, bias=rest[:, 0:1], scale=-1.0)
+
+        def turn_mean(tb):
+            turned = psum_flip.tile([P, P], BF16, tag="flip", name="turned")
+            nc.tensor.transpose(turned[:], stat_rows[:], ident_bf[:])
+            mean_lhs[tb] = stat.tile([P, P], BF16, name="mean_lhs")
+            nc.scalar.copy(out=mean_lhs[tb][:], in_=turned[:])
+
+        flips_b = {}
+
+        def turn_scaled(g):
+            j = g % O_TILES
+            if j % 7 < 3:
+                flips_b[g] = psum_mx.tile([P, FREQ, P], F32, tag="product", name="flipped")
+            else:
+                flips_b[g] = psum_flip.tile([P, FREQ, P], F32, tag="flip", name="flipped")
+            for f in range(FREQ):
+                for j, copy in enumerate(scaled[g]):
+                    nc.tensor.matmul(
+                        out=flips_b[g][:, f, :], lhsT=copy[:, f * P : (f + 1) * P], rhs=ident[:],
+                        is_transpose=True, start=f == 0 and j == 0, stop=False,
+                    )
+
+            gamma_part = gamma_bc[:, (g % O_TILES) * BANK : (g % O_TILES + 1) * BANK]
+            nc.tensor.matmul(
+                out=flips_b[g][:], lhsT=mean_lhs[g // O_TILES][:], rhs=gamma_part.rearrange("p (o f) -> p f o", f=FREQ), start=False, stop=True
+            )
+
+        def leave(g):
+            norm_of(g)
+            part = slice((g % PIECE_TILES) * BANK, (g % PIECE_TILES + 1) * BANK)
+            beta_part = beta_bc[:, (g % O_TILES) * BANK : (g % O_TILES + 1) * BANK]
+            nc.vector.scalar_tensor_tensor(
+                out=norms[g // PIECE_TILES][:, part].rearrange("p (o f) -> p o f", f=FREQ),
+                in0=flips_b[g][:].rearrange("p f o -> p o f"),
+                scalar=signed_rstd[g // O_TILES][:, 0:1],
+                in1=beta_part.rearrange("p (o f) -> p o f", f=FREQ),
+                op0=ALU.mult,
+                op1=ALU.add,
+            )
+
         jobs = []
 
         def at(step, rank, job, *args):
@@ -434,6 +480,7 @@ def tile_unified2dattentiononframe_pa_kernel(
             at(first - 0.5, 6.5, quantise_w, i)
             first += n
         at(-10, 0, slope_constants)
+        at(12, 9.5, lambda: nc.gpsimd.tensor_copy(out=gamma_cols[:], in_=gamma_cols_bf[:]))
         at(1, 3.5, bias_constants)
         at(-5, 0, group_x, 0, [nc.vector.tensor_copy, nc.scalar.copy])
         at(-4, 0, quantise_x, 0)
@@ -445,49 +492,41 @@ def tile_unified2dattentiononframe_pa_kernel(
             i = g % O_TILES
             q = g // TG * TG + (TG - 1)
             base = tb * O_TILES + O_TILES - 1 + AT_MEAN
-            j = i if tb != LAST else (i - EARLY) % O_TILES
-            squares = O_TILES if tb != LAST else O_TILES - EARLY
-            pace = ((.75,.75,.75,1))[tb]
-            turn = base + 1 + (j // TG) * TG * pace
-            ready = base + 1 + (squares - TG) * pace + 1
+            fold = fold_tile(g)
+            pace = PB[tb]
+            turn = base + 1 + (i // TG) * TG * pace
+            ready = base + 1 + (O_TILES - TG) * pace + 1
             at(q, 3, multiply, g)
             at(q + AT_BIAS + (g % TG) - TG + 1, 4, add_bias, g)
             if KIND(g) == "S":
                 at(q + AT_BIAS + (g % TG) - TG + 1, 4.1, bend_s, g)
             else:
-                at(g + AT_PRELU, 7, prelu if KIND(g) == "V" else bend_v, g)
+                at(g + AT_P[tb], 7, prelu if KIND(g) == "V" else bend_v, g)
             at(q + AT_SUM, 2, add_to_row_sums, g)
-            if tb == TWICE:
-                turn = base + 1 + (i // TG) * TG * 0.75
-                ready = base + 1 + (O_TILES - TG) * 0.75 + 1
-                at(turn, 1, flip, g)
-                at(turn + (g % TG) * 0.75, 5, square, g)
-                turn = base + 6 + (i // TG) * TG * 1
-                pace = 1
-                at(turn, 1, flip, g)
-            elif j < squares:
-                at(turn, 1, flip, g)
-                at(turn + (g % TG) * pace, 5, square, g)
+            at(turn, 1, flip, g)
+            at(turn + (g % TG) * pace, 5, square, g)
+            if fold:
+                at(base + GP_AT + i * GP_PACE, 7.6 if GP_ENG[i % len(GP_ENG)] == "V" else 5.1, scale_rows, g, GP_ENG[i % len(GP_ENG)])
+                last = ready + 1.5 + i
+                at(base + PRE + i * GP_PACE if i < 3 else ready + 0.7 if i < 7 else last - 6, 1.5, turn_scaled, g)
+                at(last, 7.5, leave, g)
             else:
-                at(turn, 1, flip, g)
-                early = TILES + 0 + (i // TG) * TG
-                at(early, 1.5, early_flip, g)
-                at(early + g % TG, 5.2, early_square, g)
-            at(turn + (g % TG) * pace + 0, 7.5, gain, g)
-            last = ready + (1 if tb != TWICE else 1) + 1 + j * ((1, 1, 1, 1))[tb]
-            at(last, 7.7, scale_shift, g)
+                at(turn + (g % TG) * pace, 7.5, gain, g)
+                last = ready + 1 + SH[tb] + i * SHP[tb]
+                at(last, 7.7, scale_shift, g)
             if g % PIECE_TILES == 0:
                 piece_end = 0
             piece_end = max(piece_end, last)
-            if (tb, i // PIECE_TILES) in ((3,0),(3,1),(3,2),(3,3)):
+            if (tb, i // PIECE_TILES) in ((3, 3),):
                 at(last, 9, store_tile, g)
             elif g % PIECE_TILES == PIECE_TILES - 1:
                 at(piece_end, 9, store, g // PIECE_TILES)
             if i == O_TILES - 1:
                 at(base, 4.5, mean_of_block, tb)
                 at(ready, 5.5, deviation_of_block, tb)
-                at(ready + (1 if tb != TWICE else 1), 6.5, rstd_of_block, tb)
-        if EARLY:
-            at(LAST * O_TILES + EARLY - 1 + AT_MEAN, 4.5, early_mean)
+                at(ready + 1, 6.5, rstd_of_block, tb)
+                if fold_tile(g):
+                    at(base, 4.6, mean_rows, tb)
+                    at(base + MR, 1.4, turn_mean, tb)
         for step, rank, index, job, args in sorted(jobs, key=lambda j: j[:3]):
             job(*args)

from contextlib import ExitStack

import concourse.mybir as mybir
from concourse.masks import make_identity

F32 = mybir.dt.float32
BF16 = mybir.dt.bfloat16
U32 = mybir.dt.uint32
U8 = mybir.dt.uint8
FP8X4 = mybir.dt.float8_e4m3fn_x4
ALU = mybir.AluOpType
ACT = mybir.ActivationFunctionType

P = 128
PACK = 4
CIN = 512
COUT = 1536
FREQ = 4
T = 512
HEADS = 8
HEAD_DIM = 256
EPS = 1e-5
BANK = 512
O_TILES = COUT // P
T_BLOCKS = T // P
ROW = COUT * FREQ
PIECE_TILES = 3
PIECE_COLS = PIECE_TILES * BANK
PIECE_HEADS = PIECE_COLS // (3 * HEAD_DIM)
TILES = T_BLOCKS * O_TILES
FLOPS = 2 * COUT * CIN * FREQ * T

W_GROUPS = (1,1,2,2,2,2,2)
AT_BIAS = 2
AT_PRELU = 3
AT_SUM = 5
AT_MEAN = 5
TG = 2
NB = 8
BB = 14
AB = 22
AT_P = (3, 3, 3, 3)
KB = ("V", "V", "2VS", "2VS")
KIND = lambda g: KB[g // O_TILES][g % len(KB[g // O_TILES])]
FOLD2 = 12
FOLD3 = 0
PB = (0.75, 0.75, 0.75, 0.5)
SH = (1, 1, 1, 1)
SHP = (1, 1, 1, 1)
GP_AT = 1
PRE = 5
MR = 2
GP_PACE = 1
GP_ENG = "VVS"


def fold_tile(g):
    return (g // O_TILES == 3 and g % O_TILES >= FOLD3) or (g // O_TILES == 2 and g % O_TILES >= FOLD2)


XS = lambda nc, b: [nc.scalar.copy, nc.vector.tensor_copy] if b == 1 else [nc.vector.tensor_copy]
XPOS = (7,17,23)


def tile_unified2dattentiononframe_pa_kernel(
    tc, x, qkv_w, qkv_b, qkv_alpha, qkv_gamma, qkv_beta, out_0, out_1, out_2
):
    nc = tc.nc
    outs = (out_0, out_1, out_2)

    with ExitStack() as stack:
        stack.enter_context(tc.manual_schedule(engines={mybir.EngineType.PE}))
        const = stack.enter_context(tc.tile_pool(name="const", bufs=1))
        w_load = stack.enter_context(tc.tile_pool(name="w_load", bufs=1))
        group = stack.enter_context(tc.tile_pool(name="group", bufs=2))
        signed_pool = stack.enter_context(tc.tile_pool(name="signed", bufs=4))
        bend_pool = stack.enter_context(tc.tile_pool(name="bend", bufs=BB))
        act_pool = stack.enter_context(tc.tile_pool(name="act", bufs=AB))
        waste_pool = stack.enter_context(tc.tile_pool(name="waste", bufs=2))
        norm_pool = stack.enter_context(tc.tile_pool(name="norm", bufs=NB))
        stat = stack.enter_context(tc.tile_pool(name="stat", bufs=3))
        psum_mx = stack.enter_context(tc.psum_pool(name="psum_mx", bufs=3))
        psum_sum = stack.enter_context(tc.psum_pool(name="psum_sum", bufs=1))
        psum_flip = stack.enter_context(tc.psum_pool(name="psum_flip", bufs=8 - 3 - 1))

        x_rows = x[0].rearrange("(p k) f t -> p (k f) t", k=PACK)
        alpha_bf = const.tile([P, 1], BF16)
        bias_rows_bf = const.tile([P, P], BF16)
        nc.vector.memset(bias_rows_bf[:], 0.0)
        w_raw = []

        def load_w(i):
            first = sum(W_GROUPS[:i])
            raw = w_load.tile([P, W_GROUPS[i], CIN], BF16, name="w_raw%d" % i)
            rows = qkv_w[first * P : (first + W_GROUPS[i]) * P, :]
            nc.sync.dma_start(out=raw[:], in_=rows.rearrange("(a p) c -> p a c", p=P))
            w_raw.append(raw)

        load_w(0)
        x_raw0 = []
        for half in range(2):
            raw = const.tile([P, PACK, 2, P], BF16, name="x_raw0_%d" % half)
            nc.sync.dma_start(
                out=raw[:],
                in_=x[0].rearrange("(p k) f t -> p k f t", k=PACK)[:, :, 2 * half : 2 * half + 2, 0:P],
            )
            x_raw0.append(raw)
        nc.sync.dma_start(out=alpha_bf[:], in_=qkv_alpha.partition_broadcast(P))
        load_w(1)
        load_w(2)
        nc.sync.dma_start(out=bias_rows_bf[0:O_TILES, :], in_=qkv_b.rearrange("(a p) -> a p", p=P))
        for i in range(3, len(W_GROUPS)):
            load_w(i)

        x_rest = const.tile([P, PACK * FREQ, T - P], BF16)
        nc.sync.dma_start(out=x_rest[:], in_=x_rows[:, :, P:T])
        gamma_bc = const.tile([P, ROW], BF16)
        beta_bc = const.tile([P, ROW], BF16)
        gamma_cols_bf = const.tile([P, O_TILES, FREQ], BF16)
        gamma_cols = const.tile([P, O_TILES, FREQ], F32)
        stat_rows = const.tile([P, P], BF16)
        nc.gpsimd.memset(stat_rows[:], 0.0)
        ident_bf = const.tile([P, P], BF16)
        make_identity(nc, ident_bf[:])
        nc.sync.dma_start(out=gamma_bc[:], in_=qkv_gamma.rearrange("a o b f -> (a o b f)").partition_broadcast(P))
        nc.sync.dma_start(out=beta_bc[:], in_=qkv_beta.rearrange("a o b f -> (a o b f)").partition_broadcast(P))

        nc.sync.dma_start(out=gamma_cols_bf[:], in_=qkv_gamma.rearrange("a (i p) b f -> p i (a b f)", p=P))

        ident = const.tile([P, P], F32)
        make_identity(nc, ident[:])
        one = const.tile([P, 1], F32)
        nc.vector.memset(one[:], 1.0)
        one_root = const.tile([P, 1], F32)
        nc.scalar.activation(out=one_root[:], in_=one[:], func=ACT.Sqrt)
        eps = const.tile([P, 1], F32)
        nc.vector.memset(eps[:], EPS)

        def slope_constants():
            nc.gpsimd.tensor_copy(out=alpha[:], in_=alpha_bf[:])
            nc.gpsimd.tensor_scalar(out=sign[:], in0=alpha[:], scalar1=1.0, scalar2=-2.0, op0=ALU.is_gt, op1=ALU.mult)
            nc.gpsimd.tensor_scalar(out=sign[:], in0=sign[:], scalar1=1.0, scalar2=1.0, op0=ALU.add, op1=ALU.mult)
            nc.gpsimd.tensor_scalar(out=bend[:], in0=alpha[:], scalar1=-1.0, scalar2=1.0, op0=ALU.add, op1=ALU.mult)
            nc.gpsimd.tensor_tensor(out=signed_bend[:], in0=bend[:], in1=sign[:], op=ALU.mult)
            nc.gpsimd.tensor_copy(out=bias_rows[:], in_=bias_rows_bf[:])

        def bias_constants():
            bias_cols = psum_flip.tile([P, P], F32, tag="flip")
            nc.tensor.transpose(bias_cols[:], bias_rows[:], ident[:])
            nc.scalar.activation(out=signed_bias[:], in_=bias_cols[:, 0:O_TILES], func=ACT.Copy, scale=sign[:, 0:1])
            nc.gpsimd.tensor_scalar(
                out=bend_bias[:], in0=signed_bias[:], scalar1=bend[:, 0:1], scalar2=0.0, op0=ALU.mult, op1=ALU.add
            )

        alpha = const.tile([P, 1], F32)
        sign = const.tile([P, 1], F32)
        bend = const.tile([P, 1], F32)
        signed_bend = const.tile([P, 1], F32)
        bend_bias = const.tile([P, O_TILES], F32)
        bias_rows = const.tile([P, P], F32)
        signed_bias = const.tile([P, O_TILES], F32)

        w_codes = const.tile([P, COUT], U32, align_bytes=64)
        w_scales = const.tile([P, COUT], U8, align_bytes=64)
        w_grouped = {}

        w_flipped = {}

        def flip_w(i):
            n = W_GROUPS[i]
            w_flipped[i] = []
            words = w_raw[i][:].bitcast(F32).rearrange("p a (q u) -> p a u q", u=2)
            for a0 in range(0, n, 2):
                m = min(2, n - a0)
                flipped = psum_flip.tile([P, m, 2, P], F32, tag="flip", name="w_flipped")
                for a in range(m):
                    for u in range(2):
                        nc.tensor.transpose(flipped[:, a, u, :], words[:, a0 + a, u, :], ident[:])
                w_flipped[i].append((a0, m, flipped))

        def copy_w(i, eng):
            grouped = group.tile([P, 2 * P, PACK], BF16, align_bytes=64, name="w_grouped")
            w_grouped[i] = grouped
            grouped_words = grouped[:].bitcast(F32)
            for a0, m, flipped in w_flipped[i]:
                dst = grouped_words[:, a0 * P : (a0 + m) * P, :]
                eng(
                    out=dst.rearrange("p (a o) u -> p a o u", a=m),
                    in_=flipped[:].rearrange("p a u o -> p a o u"),
                )

        def quantise_w(i):
            n = W_GROUPS[i]
            first = sum(W_GROUPS[:i])
            cols = slice(first * P, (first + n) * P)
            nc.vector.quantize_mx(
                out=w_codes[:, cols].bitcast(FP8X4),
                scales=w_scales[:, cols],
                in_=w_grouped[i][:, 0 : n * P, :].rearrange("p o k -> p (o k)"),
            )

        x_codes = const.tile([P, T_BLOCKS, BANK], U32, align_bytes=64)
        x_scales = const.tile([P, T_BLOCKS, BANK], U8, align_bytes=64)
        x_grouped = {}

        def group_x(tb, engs):
            grouped = group.tile([P, BANK, PACK], BF16, align_bytes=64, name="x_grouped")
            x_grouped[tb] = grouped
            dst = grouped[:].rearrange("p (f t) k -> p f t k", f=FREQ)
            n = FREQ // len(engs)
            for f in range(FREQ):
                if tb == 0:
                    src = x_raw0[f // 2][:, :, f % 2, :]
                else:
                    src = x_rest[:].rearrange("p (k f) t -> p k f t", k=PACK)[:, :, f, (tb - 1) * P : tb * P]
                engs[f // n](
                    out=dst[:, f].rearrange("p (c i) k -> p c k i", i=4),
                    in_=src.rearrange("p k (c i) -> p c k i", i=4),
                )

        def quantise_x(tb):
            nc.vector.quantize_mx(
                out=x_codes[:, tb, :].bitcast(FP8X4),
                scales=x_scales[:, tb, :],
                in_=x_grouped[tb][:].rearrange("p n k -> p (n k)"),
            )

        products = {}
        signeds = {}
        acts = {}
        flips = {}
        norms = {}
        pairs = {}
        row_sums = {}

        def sum_group(g):
            tb = g // O_TILES
            first = tb * O_TILES
            last = first + O_TILES - 1
            return first, last

        neg_mean = {}
        square_sums = {}
        signed_deviation = {}
        signed_rstd = {}

        def multiply(g):
            o_cols = slice((g % O_TILES) * P, (g % O_TILES + 1) * P)
            products[g] = psum_mx.tile([P, BANK], F32, tag="product", name="product")
            nc.tensor.matmul_mx(
                out=products[g][:],
                lhsT=w_codes[:, o_cols].bitcast(FP8X4),
                lhsT_scale=w_scales[:, o_cols],
                rhs=x_codes[:, g // O_TILES, :].bitcast(FP8X4),
                rhs_scale=x_scales[:, g // O_TILES, :],
                start=True,
                stop=True,
            )

        parts = {}

        def add_bias(g):
            if KIND(g) == "V":
                signeds[g] = signed_pool.tile([P, BANK], F32, name="signed")
            else:
                signeds[g] = act_pool.tile([P, BANK], F32, name="act")
            nc.scalar.activation(
                out=signeds[g][:],
                in_=products[g][:],
                func=ACT.Identity,
                bias=signed_bias[:, g % O_TILES : g % O_TILES + 1],
                scale=sign[:, 0:1],
            )

        def bend_s(g):
            bends = bend_pool.tile([P, BANK], F32, name="bends")
            nc.scalar.activation(out=bends[:], in_=products[g][:], func=ACT.Relu, bias=bend_bias[:, g % O_TILES : g % O_TILES + 1], scale=signed_bend[:, 0:1])
            parts[g] = [signeds[g], bends]

        def bend_v(g):
            bends = bend_pool.tile([P, BANK], F32, name="bends")
            nc.vector.tensor_scalar(out=bends[:], in0=signeds[g][:], scalar1=bend[:, 0:1], scalar2=0.0, op0=ALU.mult, op1=ALU.max)
            parts[g] = [signeds[g], bends]

        def prelu(g):
            acts[g] = act_pool.tile([P, BANK], F32, name="act")
            nc.vector.scalar_tensor_tensor(
                out=acts[g][:], in0=signeds[g][:], scalar=alpha[:, 0:1], in1=signeds[g][:], op0=ALU.mult, op1=ALU.max
            )
            parts[g] = [acts[g]]

        def add_to_row_sums(g):
            first, last = sum_group(g)
            if g == first:
                row_sums[g] = psum_sum.tile([P, P], F32, name="row_sums")
            for j, part in enumerate(parts[g]):
                for f in range(FREQ):
                    nc.tensor.matmul(
                        out=row_sums[first][:],
                        lhsT=part[:, f * P : (f + 1) * P],
                        rhs=ident[:],
                        is_transpose=True,
                        start=(g == first and j == 0 and f == 0),
                        stop=(g == last and j == len(parts[g]) - 1 and f == FREQ - 1),
                    )

        def mean_of_block(tb):
            square_sums[tb] = stat.tile([P, O_TILES + 1], F32, name="square_sums")
            mean_tile = stat.tile([P, 1], F32, name="neg_mean")
            neg_mean[tb] = mean_tile[:, 0:1]
            waste = waste_pool.tile([P, P], BF16, name="waste_mean")
            nc.scalar.activation(
                out=waste[:], in_=row_sums[tb * O_TILES][:], func=ACT.Copy, scale=-1.0 / ROW, accum_out=neg_mean[tb]
            )

        def flip(g):
            flips[g] = psum_flip.tile([P, FREQ, P], F32, tag="flip", name="flipped")
            for f in range(FREQ):
                for j, part in enumerate(parts[g]):
                    nc.tensor.matmul(
                        out=flips[g][:, f, :],
                        lhsT=part[:, f * P : (f + 1) * P],
                        rhs=ident[:],
                        is_transpose=True,
                        start=j == 0,
                        stop=j == len(parts[g]) - 1,
                    )

        def square(g):
            waste = waste_pool.tile([P, BANK], BF16, name="waste_square")
            nc.scalar.activation(
                out=waste[:],
                in_=flips[g][:].rearrange("p f o -> p (f o)"),
                func=ACT.Square,
                bias=neg_mean[g // O_TILES],
                scale=1.0,
                accum_out=square_sums[g // O_TILES][:, g % O_TILES : g % O_TILES + 1],
            )

        def gain(g):
            norm_of(g)
            part = slice((g % PIECE_TILES) * BANK, (g % PIECE_TILES + 1) * BANK)
            gamma_part = gamma_bc[:, (g % O_TILES) * BANK : (g % O_TILES + 1) * BANK]
            nc.vector.scalar_tensor_tensor(
                out=norms[g // PIECE_TILES][:, part].rearrange("p (o f) -> p o f", f=FREQ),
                in0=flips[g][:].rearrange("p f o -> p o f"),
                scalar=neg_mean[g // O_TILES],
                in1=gamma_part.rearrange("p (o f) -> p o f", f=FREQ),
                op0=ALU.add,
                op1=ALU.mult,
            )

        def deviation_of_block(tb):
            columns = O_TILES
            waste = waste_pool.tile([P, O_TILES + 1], BF16, name="waste_variance")
            variance = stat.tile([P, 1], F32)
            nc.scalar.activation(
                out=waste[:, 0:columns], in_=square_sums[tb][:, 0:columns], func=ACT.Copy, scale=1.0 / ROW, accum_out=variance[:]
            )
            deviation = stat.tile([P, 1], F32)
            nc.scalar.activation(out=deviation[:], in_=variance[:], func=ACT.Sqrt, bias=eps[:, 0:1], scale=1.0)
            sdev = stat.tile([P, 1], F32, name="signed_deviation")
            signed_deviation[tb] = sdev[:, 0:1]
            nc.scalar.activation(out=signed_deviation[tb], in_=deviation[:], func=ACT.Copy, scale=sign[:, 0:1])

        def rstd_of_block(tb):
            signed_rstd[tb] = stat.tile([P, 1], F32, name="signed_rstd")
            nc.vector.reciprocal(out=signed_rstd[tb][:], in_=signed_deviation[tb])

        def norm_of(g):
            if g // PIECE_TILES not in norms:
                norms[g // PIECE_TILES] = norm_pool.tile([P, PIECE_COLS], F32, name="norm")
            return norms[g // PIECE_TILES]

        def store_tile(g):
            tb = g // O_TILES
            for half in range(2):
                segment = 2 * (g % O_TILES) + half
                column = (2 * (g % PIECE_TILES) + half) * HEAD_DIM
                nc.sync.dma_start(
                    out=outs[segment % 3][0, segment // 3, tb * P : (tb + 1) * P, :],
                    in_=norms[g // PIECE_TILES][:, column : column + HEAD_DIM],
                )

        def store(piece):
            tb = piece // (O_TILES // PIECE_TILES)
            s = piece % (O_TILES // PIECE_TILES)
            split = norms[piece][:].rearrange("p (h w d) -> p h w d", h=PIECE_HEADS, w=3)
            for w, out_w in enumerate(outs):
                rows = out_w[0, s * PIECE_HEADS : (s + 1) * PIECE_HEADS, tb * P : (tb + 1) * P, :]
                nc.sync.dma_start(out=rows.rearrange("h t d -> t h d"), in_=split[:, :, w, :])

        def scale_shift(g):
            norm = norms[g // PIECE_TILES]
            part = slice((g % PIECE_TILES) * BANK, (g % PIECE_TILES + 1) * BANK)
            nc.vector.scalar_tensor_tensor(
                out=norm[:, part],
                in0=norm[:, part],
                scalar=signed_rstd[g // O_TILES][:, 0:1],
                in1=beta_bc[:, (g % O_TILES) * BANK : (g % O_TILES + 1) * BANK],
                op0=ALU.mult,
                op1=ALU.add,
            )


        scaled = {}

        def scale_rows(g, eng):
            assert g in flips
            scaled[g] = []
            for whole in parts[g]:
                copy = whole
                scaled[g].append(copy)
                for f in range(FREQ):
                    part = slice(f * P, (f + 1) * P)
                    col = gamma_cols[:, g % O_TILES, f : f + 1]
                    if eng == "V":
                        nc.vector.tensor_scalar(out=copy[:, part], in0=whole[:, part], scalar1=col, scalar2=0.0, op0=ALU.mult, op1=ALU.add)
                    else:
                        nc.scalar.activation(out=copy[:, part], in_=whole[:, part], func=ACT.Copy, scale=col)

        mean_lhs = {}

        def mean_rows(tb):
            rest = stat.tile([P, 1], F32, name="rest")
            hi, mid, lo = (stat_rows[:, 2 * i : 2 * i + 1] for i in range(3))
            nc.scalar.activation(out=hi, in_=neg_mean[tb], func=ACT.Copy)
            nc.scalar.activation(out=rest[:], in_=hi, func=ACT.Identity, bias=neg_mean[tb], scale=-1.0)
            nc.scalar.activation(out=mid, in_=rest[:], func=ACT.Copy)
            nc.scalar.activation(out=lo, in_=mid, func=ACT.Identity, bias=rest[:, 0:1], scale=-1.0)

        def turn_mean(tb):
            turned = psum_flip.tile([P, P], BF16, tag="flip", name="turned")
            nc.tensor.transpose(turned[:], stat_rows[:], ident_bf[:])
            mean_lhs[tb] = stat.tile([P, P], BF16, name="mean_lhs")
            nc.scalar.copy(out=mean_lhs[tb][:], in_=turned[:])

        flips_b = {}

        def turn_scaled(g):
            j = g % O_TILES
            if j % 7 < 3:
                flips_b[g] = psum_mx.tile([P, FREQ, P], F32, tag="product", name="flipped")
            else:
                flips_b[g] = psum_flip.tile([P, FREQ, P], F32, tag="flip", name="flipped")
            for f in range(FREQ):
                for j, copy in enumerate(scaled[g]):
                    nc.tensor.matmul(
                        out=flips_b[g][:, f, :], lhsT=copy[:, f * P : (f + 1) * P], rhs=ident[:],
                        is_transpose=True, start=f == 0 and j == 0, stop=False,
                    )

            gamma_part = gamma_bc[:, (g % O_TILES) * BANK : (g % O_TILES + 1) * BANK]
            nc.tensor.matmul(
                out=flips_b[g][:], lhsT=mean_lhs[g // O_TILES][:], rhs=gamma_part.rearrange("p (o f) -> p f o", f=FREQ), start=False, stop=True
            )

        def leave(g):
            norm_of(g)
            part = slice((g % PIECE_TILES) * BANK, (g % PIECE_TILES + 1) * BANK)
            beta_part = beta_bc[:, (g % O_TILES) * BANK : (g % O_TILES + 1) * BANK]
            nc.vector.scalar_tensor_tensor(
                out=norms[g // PIECE_TILES][:, part].rearrange("p (o f) -> p o f", f=FREQ),
                in0=flips_b[g][:].rearrange("p f o -> p o f"),
                scalar=signed_rstd[g // O_TILES][:, 0:1],
                in1=beta_part.rearrange("p (o f) -> p o f", f=FREQ),
                op0=ALU.mult,
                op1=ALU.add,
            )

        jobs = []

        def at(step, rank, job, *args):
            jobs.append((step, rank, len(jobs), job, args))

        first = 0
        for i, n in enumerate(W_GROUPS):
            at(first - 2, 0, flip_w, i)
            at(first - 1.5, 3.5, copy_w, i, nc.scalar.copy if i % 2 == 0 else nc.vector.tensor_copy)
            at(first - 0.5, 6.5, quantise_w, i)
            first += n
        at(-10, 0, slope_constants)
        at(12, 9.5, lambda: nc.gpsimd.tensor_copy(out=gamma_cols[:], in_=gamma_cols_bf[:]))
        at(1, 3.5, bias_constants)
        at(-5, 0, group_x, 0, [nc.vector.tensor_copy, nc.scalar.copy])
        at(-4, 0, quantise_x, 0)
        for b in (1, 2, 3):
            at(XPOS[b - 1], 8, group_x, b, XS(nc, b))
            at(XPOS[b - 1] + 3, 9, quantise_x, b)
        for g in range(TILES):
            tb = g // O_TILES
            i = g % O_TILES
            q = g // TG * TG + (TG - 1)
            base = tb * O_TILES + O_TILES - 1 + AT_MEAN
            fold = fold_tile(g)
            pace = PB[tb]
            turn = base + 1 + (i // TG) * TG * pace
            ready = base + 1 + (O_TILES - TG) * pace + 1
            at(q, 3, multiply, g)
            at(q + AT_BIAS + (g % TG) - TG + 1, 4, add_bias, g)
            if KIND(g) == "S":
                at(q + AT_BIAS + (g % TG) - TG + 1, 4.1, bend_s, g)
            else:
                at(g + AT_P[tb], 7, prelu if KIND(g) == "V" else bend_v, g)
            at(q + AT_SUM, 2, add_to_row_sums, g)
            at(turn, 1, flip, g)
            at(turn + (g % TG) * pace, 5, square, g)
            if fold:
                at(base + GP_AT + i * GP_PACE, 7.6 if GP_ENG[i % len(GP_ENG)] == "V" else 5.1, scale_rows, g, GP_ENG[i % len(GP_ENG)])
                last = ready + 1.5 + i
                at(base + PRE + i * GP_PACE if i < 3 else ready + 0.7 if i < 7 else last - 6, 1.5, turn_scaled, g)
                at(last, 7.5, leave, g)
            else:
                at(turn + (g % TG) * pace, 7.5, gain, g)
                last = ready + 1 + SH[tb] + i * SHP[tb]
                at(last, 7.7, scale_shift, g)
            if g % PIECE_TILES == 0:
                piece_end = 0
            piece_end = max(piece_end, last)
            if (tb, i // PIECE_TILES) in ((3, 3),):
                at(last, 9, store_tile, g)
            elif g % PIECE_TILES == PIECE_TILES - 1:
                at(piece_end, 9, store, g // PIECE_TILES)
            if i == O_TILES - 1:
                at(base, 4.5, mean_of_block, tb)
                at(ready, 5.5, deviation_of_block, tb)
                at(ready + 1, 6.5, rstd_of_block, tb)
                if fold_tile(g):
                    at(base, 4.6, mean_rows, tb)
                    at(base + MR, 1.4, turn_mean, tb)
        for step, rank, index, job, args in sorted(jobs, key=lambda j: j[:3]):
            job(*args)
